import numpy as np
import ml_dtypes


def mxq(x, axis, fmt="e4m3"):
    dtype, down = {"e4m3": (ml_dtypes.float8_e4m3fn, 7), "e5m2": (ml_dtypes.float8_e5m2, 14)}[fmt]
    v = np.moveaxis(np.asarray(x, np.float32).astype(ml_dtypes.bfloat16).astype(np.float64), axis, -1)
    blocks = v.reshape(v.shape[:-1] + (-1, 32))
    amax = np.abs(blocks).max(-1, keepdims=True)
    byte = np.maximum(np.where(amax > 0, np.frexp(amax)[1] - 1 + 127, 0) - down, 1)
    scale = np.exp2(byte - 127.0)
    codes = (blocks / scale).astype(np.float32).astype(dtype).astype(np.float64)
    return np.moveaxis((codes * scale).reshape(v.shape), -1, axis)


WIDE = False


def mx_kscale(k):
    if not WIDE:
        return np.ones(k)
    levels = np.array([10, -10, 5, -5, 0])
    a = np.random.permutation(np.resize(levels, k // 512 * 4)).reshape(k // 512, 4)
    idx = np.arange(k)
    return np.exp2(a[idx // 512, idx % 128 // 32])


BF16 = ml_dtypes.bfloat16


def bf(x):
    return np.asarray(x, np.float32).astype(BF16)


def f64(x):
    return np.asarray(x).astype(np.float64)


M, N, H = 4096, 512, 512
RMIN, RMAX = 0.4, 0.99


def half_glorot(rows, cols):
    limit = np.sqrt(1.5 / ((rows + cols) / 2.0))
    return np.random.uniform(-limit, limit, (rows, cols))


def setup_inputs():
    s, t = mx_kscale(N), mx_kscale(H)
    inputs = np.random.standard_normal((M, N))
    state_re = np.random.standard_normal((M, H))
    state_im = np.random.standard_normal((M, H))
    C_re = half_glorot(H, N)
    C_im = half_glorot(H, N)
    B_re = half_glorot(N, H)
    B_im = half_glorot(N, H)
    D = np.random.standard_normal(N)
    nu = np.random.uniform(np.log(-np.log(RMAX)), np.log(-np.log(RMIN)), H)
    theta = np.random.uniform(0.0, 3.14 / 10, H)
    gamma = np.sqrt(1.0 - np.exp(-2.0 * np.exp(nu)))
    return {"inputs": bf(inputs * s), "state_re": bf(state_re * t), "state_im": bf(state_im * t),
            "B_re": bf(B_re / s[:, None]), "B_im": bf(B_im / s[:, None]),
            "C_re": bf(C_re / t[:, None]), "C_im": bf(C_im / t[:, None]),
            "D": bf(D / s), "nu": bf(nu), "theta": bf(theta), "gamma": bf(gamma * t)}


def reference(inputs, state_re, state_im, B_re, B_im, C_re, C_im, D, nu, theta, gamma):
    u = f64(inputs)
    mag = np.exp(-np.exp(f64(nu)))
    lam_re = mag * np.cos(f64(theta))
    lam_im = mag * np.sin(f64(theta))
    uq = mxq(u, 1, "e4m3")
    new_u_re = f64(gamma) * (uq @ mxq(f64(B_re), 0, "e4m3"))
    new_u_im = f64(gamma) * (uq @ mxq(f64(B_im), 0, "e4m3"))
    x_re = f64(state_re) * lam_re - f64(state_im) * lam_im + new_u_re
    x_im = f64(state_re) * lam_im + f64(state_im) * lam_re + new_u_im
    y = (mxq(x_re, 1, "e4m3") @ mxq(f64(C_re), 0, "e4m3")) - (mxq(x_im, 1, "e4m3") @ mxq(f64(C_im), 0, "e4m3")) + f64(D) * u
    return y, x_re, x_im

@@ -1,0 +1,324 @@
+from contextlib import ExitStack
+import math
+
+import concourse.mybir as mybir
+from concourse.masks import make_identity
+
+F32 = mybir.dt.float32
+BF16 = mybir.dt.bfloat16
+U32 = mybir.dt.uint32
+U8 = mybir.dt.uint8
+I32 = mybir.dt.int32
+FP8X4 = mybir.dt.float8_e4m3fn_x4
+ALU = mybir.AluOpType
+ACTF = mybir.ActivationFunctionType
+
+P = 128
+ROWS = 4096
+WIDTH = 512
+R = 512
+J = R // P
+NCH = ROWS // R
+FLOPS = 4 * 2 * ROWS * WIDTH * WIDTH
+
+TWO_PI_HI = 6.28125
+TWO_PI_LO = 2.0 * math.pi - 6.28125
+
+
+def tile_linearrecurrentunitcell_t_kernel(
+    tc, inputs, state_re, state_im, B_re, B_im, C_re, C_im, D, nu, theta, gamma, out_0, out_1, out_2
+):
+    nc = tc.nc
+    with ExitStack() as ctx:
+        const = ctx.enter_context(tc.tile_pool(name="const", bufs=1))
+        io = ctx.enter_context(tc.tile_pool(name="io", bufs=3))
+        work = ctx.enter_context(tc.tile_pool(name="work", bufs=2))
+        psum = ctx.enter_context(tc.psum_pool(name="psum", bufs=1))
+
+        pr_nu = const.tile([P, 4], BF16, name="pr_nu")
+        pr_th = const.tile([P, 4], BF16, name="pr_th")
+        pr_ga = const.tile([P, 4], BF16, name="pr_ga")
+        with nc.allow_non_contiguous_dma(reason="three vectors of 512 values, two neighbours a piece"):
+            for dst, vec in ((pr_nu, nu), (pr_th, theta), (pr_ga, gamma)):
+                nc.scalar.dma_start(
+                    out=dst[:].rearrange("p (u e) -> p u e", u=2),
+                    in_=vec.rearrange("(u q e) -> q u e", u=2, e=2),
+                )
+        dbc = const.tile([P, WIDTH], BF16, name="dbc")
+        nc.scalar.dma_start(out=dbc[:], in_=D.partition_broadcast(P))
+
+        u_t = {}
+        sre_t = {}
+        sim_t = {}
+
+        def load_u(c):
+            u_sb = io.tile([P, J * WIDTH], BF16, tag="u", name="u_sb")
+            nc.sync.dma_start(out=u_sb[:], in_=inputs[c * R:(c + 1) * R, :].rearrange("(i j) k -> i (j k)", j=J))
+            u_t[c] = u_sb
+
+        def load_s(c):
+            sre = io.tile([P, J * WIDTH], BF16, tag="sre", name="sre")
+            nc.sync.dma_start(out=sre[:], in_=state_re[c * R:(c + 1) * R, :].rearrange("(i j) k -> i (j k)", j=J))
+            sre_t[c] = sre
+            sim = io.tile([P, J * WIDTH], BF16, tag="sim", name="sim")
+            nc.sync.dma_start(out=sim[:], in_=state_im[c * R:(c + 1) * R, :].rearrange("(i j) k -> i (j k)", j=J))
+            sim_t[c] = sim
+
+        def load_w(w, nm):
+            raw = const.tile([P, 4 * WIDTH], BF16, name="raw_" + nm)
+            nc.sync.dma_start(
+                out=raw[:].rearrange("p (u x) -> p u x", u=2),
+                in_=w.rearrange("(u q e) c -> q u (e c)", u=2, e=2),
+            )
+            return raw
+
+        load_u(0)
+        raw_bre = load_w(B_re, "bre")
+        raw_bim = load_w(B_im, "bim")
+        load_s(0)
+        raw_cre = load_w(C_re, "cre")
+        raw_cim = load_w(C_im, "cim")
+        load_u(1)
+        load_s(1)
+        load_u(2)
+        load_s(2)
+
+        ident = const.tile([P, P], F32, name="ident")
+        make_identity(nc, ident[:])
+
+        def small(nm, dt=F32):
+            return const.tile([P, 4], dt, name=nm)
+
+        e1 = small("e1")
+        nc.scalar.activation(out=e1[:], in_=pr_nu[:], func=ACTF.Exp)
+        mag = small("mag")
+        nc.scalar.activation(out=mag[:], in_=e1[:], func=ACTF.Exp, scale=-1.0)
+        thf = small("thf")
+        nc.vector.tensor_copy(out=thf[:], in_=pr_th[:])
+        gam = small("gam")
+        nc.vector.tensor_copy(out=gam[:], in_=pr_ga[:])
+        kq = small("kq")
+        nc.vector.tensor_scalar_mul(out=kq[:], in0=thf[:], scalar1=1.0 / (2.0 * math.pi))
+        ki = small("ki", I32)
+        nc.vector.tensor_copy(out=ki[:], in_=kq[:])
+        kf = small("kf")
+        nc.vector.tensor_copy(out=kf[:], in_=ki[:])
+        r1 = small("r1")
+        nc.vector.scalar_tensor_tensor(out=r1[:], in0=kf[:], scalar=-TWO_PI_HI, in1=thf[:], op0=ALU.mult, op1=ALU.add)
+        r2 = small("r2")
+        nc.vector.scalar_tensor_tensor(out=r2[:], in0=kf[:], scalar=-TWO_PI_LO, in1=r1[:], op0=ALU.mult, op1=ALU.add)
+        sa = small("sa")
+        nc.scalar.activation(out=sa[:], in_=r2[:], func=ACTF.Sin, scale=0.5)
+        sb = small("sb")
+        nc.scalar.activation(out=sb[:], in_=r2[:], func=ACTF.Sin, scale=0.25)
+        sa2 = small("sa2")
+        nc.vector.tensor_tensor(out=sa2[:], in0=sa[:], in1=sa[:], op=ALU.mult)
+        cosr = small("cosr")
+        nc.vector.tensor_scalar(out=cosr[:], in0=sa2[:], scalar1=-2.0, scalar2=1.0, op0=ALU.mult, op1=ALU.add)
+        sb2 = small("sb2")
+        nc.vector.tensor_tensor(out=sb2[:], in0=sb[:], in1=sb[:], op=ALU.mult)
+        ch2 = small("ch2")
+        nc.vector.tensor_scalar(out=ch2[:], in0=sb2[:], scalar1=-4.0, scalar2=2.0, op0=ALU.mult, op1=ALU.add)
+        sinr = small("sinr")
+        nc.vector.tensor_tensor(out=sinr[:], in0=sa[:], in1=ch2[:], op=ALU.mult)
+        lam_re = small("lam_re")
+        nc.vector.tensor_tensor(out=lam_re[:], in0=mag[:], in1=cosr[:], op=ALU.mult)
+        lam_im = small("lam_im")
+        nc.vector.tensor_tensor(out=lam_im[:], in0=mag[:], in1=sinr[:], op=ALU.mult)
+        nlam_im = small("nlam_im")
+        nc.vector.tensor_scalar_mul(out=nlam_im[:], in0=lam_im[:], scalar1=-1.0)
+
+        def codes(nm):
+            cd = const.tile([P, WIDTH], U32, name="cd_" + nm, align_bytes=64)
+            sc = const.tile([P, WIDTH], U8, name="sc_" + nm, align_bytes=64)
+            return cd, sc
+
+        def prep_b(raw, nm):
+            g = work.tile([P, 4 * WIDTH], BF16, tag="gw", name="g_" + nm, align_bytes=64)
+            src = raw[:].rearrange("p (t u q e) -> p u e q t", t=4, u=2, e=2)
+            dst = g[:].rearrange("p (u e q t) -> p u e q t", u=2, e=2, t=4)
+            for uu in range(2):
+                nc.vector.tensor_copy(out=dst[:, uu], in_=src[:, uu])
+            cd, sc = codes(nm)
+            nc.vector.quantize_mx(out=cd[:].bitcast(FP8X4), scales=sc[:], in_=g[:])
+            return cd, sc
+
+        def prep_c(raw, nm, sign):
+            g = work.tile([P, 4 * WIDTH], BF16, tag="gw", name="g_" + nm, align_bytes=64)
+            nc.gpsimd.tensor_scalar(
+                out=g[:].rearrange("p (n t) -> p n t", t=4),
+                in0=raw[:].rearrange("p (t n) -> p n t", t=4),
+                scalar1=sign, scalar2=0.0, op0=ALU.mult, op1=ALU.add,
+            )
+            cd, sc = codes(nm)
+            nc.vector.quantize_mx(out=cd[:].bitcast(FP8X4), scales=sc[:], in_=g[:])
+            return cd, sc
+
+        b_cd = [prep_b(raw_bre, "bre"), prep_b(raw_bim, "bim")]
+        c_cd = [prep_c(raw_cre, "cre", 1.0), prep_c(raw_cim, "cim", -1.0)]
+
+        uq_t = {}
+        du_t = {}
+        xT_t = {}
+        xq_t = {}
+        xo_t = {}
+        yo_t = {}
+
+        def prep_u(c):
+            u_w = u_t[c][:].bitcast(F32)
+            gu = work.tile([P, 4 * R], BF16, tag="gu", name="gu", align_bytes=64)
+            gu_w = gu[:].bitcast(F32).rearrange("p (m u) -> p m u", u=2)
+            for hc in range(J // 2):
+                ut = psum.tile([P, 2, 256], F32, tag="ut", name="ut")
+                for jj in range(2):
+                    j = 2 * hc + jj
+                    for u in range(2):
+                        nc.tensor.transpose(
+                            ut[:, u, jj * P:(jj + 1) * P], u_w[:, j * 256 + u * P:j * 256 + (u + 1) * P], ident[:]
+                        )
+                nc.scalar.copy(out=gu_w[:, hc * 256:(hc + 1) * 256, :], in_=ut[:].rearrange("p u m -> p m u"))
+            uc = work.tile([P, R], U32, tag="uc", name="uc", align_bytes=64)
+            us = work.tile([P, R], U8, tag="us", name="us", align_bytes=64)
+            nc.vector.quantize_mx(out=uc[:].bitcast(FP8X4), scales=us[:], in_=gu[:])
+            uq_t[c] = (uc, us)
+
+        def skip_term(c):
+            du = work.tile([P, J, WIDTH], F32, tag="du", name="du")
+            nc.gpsimd.tensor_tensor(
+                out=du[:],
+                in0=u_t[c][:].rearrange("p (j k) -> p j k", j=J),
+                in1=dbc[:].unsqueeze(1).to_broadcast([P, J, WIDTH]),
+                op=ALU.mult,
+            )
+            du_t[c] = du
+
+        st_t = {}
+
+        def main_step(c, t):
+            u, e = divmod(t, 2)
+            if t == 0:
+                xre = work.tile([P, 4, R], F32, tag="xTre", name="xTre")
+                xim = work.tile([P, 4, R], F32, tag="xTim", name="xTim")
+                xT_t[c] = (xre, xim)
+            xre, xim = xT_t[c]
+            if e == 0:
+                pair = []
+                for src_t, tg in ((sre_t[c], "str"), (sim_t[c], "sti")):
+                    s_w = src_t[:].bitcast(F32)
+                    st = psum.tile([P, R], F32, tag=tg, name=tg)
+                    for j in range(J):
+                        nc.tensor.transpose(
+                            st[:, j * P:(j + 1) * P], s_w[:, j * 256 + u * P:j * 256 + (u + 1) * P], ident[:]
+                        )
+                    pair.append(st[:].bitcast(BF16).rearrange("p (m e) -> p m e", e=2))
+                st_t[c] = pair
+            s_re, s_im = st_t[c]
+            col = slice(t, t + 1)
+            nc.scalar.activation(out=xre[:, t, :], in_=s_re[:, :, e], func=ACTF.Copy, scale=lam_re[:, col])
+            nc.scalar.activation(out=xim[:, t, :], in_=s_re[:, :, e], func=ACTF.Copy, scale=lam_im[:, col])
+            uc, us = uq_t[c]
+            pps = []
+            for ri in range(2):
+                cd, sc = b_cd[ri]
+                pp = psum.tile([P, R], F32, tag="pp", name="pp", bufs=2)
+                nc.tensor.matmul_mx(
+                    out=pp[:],
+                    lhsT=cd[:, t * P:(t + 1) * P].bitcast(FP8X4), lhsT_scale=sc[:, t * P:(t + 1) * P],
+                    rhs=uc[:].bitcast(FP8X4), rhs_scale=us[:],
+                    start=True, stop=True,
+                )
+                pps.append(pp)
+            nc.vector.scalar_tensor_tensor(
+                out=xre[:, t, :], in0=s_im[:, :, e], scalar=nlam_im[:, col], in1=xre[:, t, :], op0=ALU.mult, op1=ALU.add
+            )
+            nc.vector.scalar_tensor_tensor(
+                out=xim[:, t, :], in0=s_im[:, :, e], scalar=lam_re[:, col], in1=xim[:, t, :], op0=ALU.mult, op1=ALU.add
+            )
+            nc.vector.scalar_tensor_tensor(
+                out=xre[:, t, :], in0=pps[0][:], scalar=gam[:, col], in1=xre[:, t, :], op0=ALU.mult, op1=ALU.add
+            )
+            nc.vector.scalar_tensor_tensor(
+                out=xim[:, t, :], in0=pps[1][:], scalar=gam[:, col], in1=xim[:, t, :], op0=ALU.mult, op1=ALU.add
+            )
+
+        gx_t = {}
+
+        def cast_x(c):
+            gs = []
+            for ri, tg in ((0, "gxre"), (1, "gxim")):
+                gx = work.tile([P, 4 * R], BF16, tag=tg, name=tg, align_bytes=64)
+                nc.gpsimd.tensor_scalar(
+                    out=gx[:].rearrange("p (m t) -> p m t", t=4),
+                    in0=xT_t[c][ri][:].rearrange("p t m -> p m t"),
+                    scalar1=1.0, scalar2=0.0, op0=ALU.mult, op1=ALU.add,
+                )
+                gs.append(gx)
+            gx_t[c] = gs
+
+        def quant_x(c):
+            qs = []
+            for ri, tg in ((0, "re"), (1, "im")):
+                xc = work.tile([P, R], U32, tag="xc" + tg, name="xc" + tg, align_bytes=64)
+                xs = work.tile([P, R], U8, tag="xs" + tg, name="xs" + tg, align_bytes=64)
+                nc.vector.quantize_mx(out=xc[:].bitcast(FP8X4), scales=xs[:], in_=gx_t[c][ri][:])
+                qs.append((xc, xs))
+            xq_t[c] = qs
+
+        def xback(c, j):
+            if j == 0:
+                xore = work.tile([P, J, WIDTH], F32, tag="xore", name="xore")
+                xoim = work.tile([P, J, WIDTH], F32, tag="xoim", name="xoim")
+                xo_t[c] = (xore, xoim)
+            for ri in range(2):
+                xn = psum.tile([P, WIDTH], F32, tag="xn", name="xn", bufs=2)
+                for t in range(4):
+                    nc.tensor.transpose(xn[:, t * P:(t + 1) * P], xT_t[c][ri][:, t, j * P:(j + 1) * P], ident[:])
+                nc.scalar.copy(
+                    out=xo_t[c][ri][:, j, :].rearrange("p (u q e) -> p u q e", u=2, e=2),
+                    in_=xn[:].rearrange("p (u e q) -> p u q e", u=2, e=2),
+                )
+
+        def ystep(c, j):
+            if j == 0:
+                yo_t[c] = work.tile([P, J, WIDTH], F32, tag="yo", name="yo")
+            yy = psum.tile([P, WIDTH], F32, tag="yy", name="yy")
+            for ri in range(2):
+                xc, xs = xq_t[c][ri]
+                cd, sc = c_cd[ri]
+                nc.tensor.matmul_mx(
+                    out=yy[:],
+                    lhsT=xc[:, j * P:(j + 1) * P].bitcast(FP8X4), lhsT_scale=xs[:, j * P:(j + 1) * P],
+                    rhs=cd[:].bitcast(FP8X4), rhs_scale=sc[:],
+                    start=(ri == 0), stop=(ri == 1),
+                )
+            nc.vector.tensor_tensor(out=yo_t[c][:, j, :], in0=yy[:], in1=du_t[c][:, j, :], op=ALU.add)
+
+        def store(dst, c, src):
+            nc.sync.dma_start(out=dst[c * R:(c + 1) * R, :].rearrange("(i j) h -> i j h", j=J), in_=src[:])
+
+        prep_u(0)
+        for c in range(NCH + 1):
+            prev = c - 1
+            if prev >= 0:
+                cast_x(prev)
+            if c < NCH:
+                skip_term(c)
+            if c + 1 < NCH:
+                prep_u(c + 1)
+            for k in range(4):
+                if c < NCH:
+                    main_step(c, k)
+                if prev >= 0:
+                    xback(prev, k)
+                    if k == 1:
+                        quant_x(prev)
+                    if k >= 2:
+                        ystep(prev, 2 * (k - 2))
+                        ystep(prev, 2 * (k - 2) + 1)
+            if prev >= 0:
+                store(out_1, prev, xo_t[prev][0])
+                store(out_2, prev, xo_t[prev][1])
+                store(out_0, prev, yo_t[prev])
+            if c + 3 < NCH:
+                load_u(c + 3)
+                load_s(c + 3)

@@ -19,10 +19,12 @@ WIDTH = 512
 R = 512
 J = R // P
 NCH = ROWS // R
+NPL = 4 * NCH
 FLOPS = 4 * 2 * ROWS * WIDTH * WIDTH
 
 TWO_PI_HI = 6.28125
 TWO_PI_LO = 2.0 * math.pi - 6.28125
+PIN = True
 
 
 def tile_linearrecurrentunitcell_t_kernel(
@@ -30,10 +32,18 @@ def tile_linearrecurrentunitcell_t_kernel(
 ):
     nc = tc.nc
     with ExitStack() as ctx:
+        if PIN:
+            ctx.enter_context(tc.manual_schedule())
         const = ctx.enter_context(tc.tile_pool(name="const", bufs=1))
         io = ctx.enter_context(tc.tile_pool(name="io", bufs=3))
         work = ctx.enter_context(tc.tile_pool(name="work", bufs=2))
         psum = ctx.enter_context(tc.psum_pool(name="psum", bufs=1))
+
+        def ok(c):
+            return 0 <= c < NCH
+
+        def okp(g):
+            return 0 <= g < NPL
 
         pr_nu = const.tile([P, 4], BF16, name="pr_nu")
         pr_th = const.tile([P, 4], BF16, name="pr_th")
@@ -51,37 +61,41 @@ def tile_linearrecurrentunitcell_t_kernel(
         sre_t = {}
         sim_t = {}
 
+        def rows_of(dram, c):
+            return dram[c * R:(c + 1) * R, :]
+
         def load_u(c):
-            u_sb = io.tile([P, J * WIDTH], BF16, tag="u", name="u_sb")
-            nc.sync.dma_start(out=u_sb[:], in_=inputs[c * R:(c + 1) * R, :].rearrange("(i j) k -> i (j k)", j=J))
+            u_sb = io.tile([P, J * WIDTH], BF16, tag="u", name="u_sb", bufs=4)
+            nc.sync.dma_start(out=u_sb[:], in_=rows_of(inputs, c).rearrange("(i j) k -> i (j k)", j=J))
             u_t[c] = u_sb
 
         def load_s(c):
             sre = io.tile([P, J * WIDTH], BF16, tag="sre", name="sre")
-            nc.sync.dma_start(out=sre[:], in_=state_re[c * R:(c + 1) * R, :].rearrange("(i j) k -> i (j k)", j=J))
+            nc.sync.dma_start(out=sre[:], in_=rows_of(state_re, c).rearrange("(i j) k -> i (j k)", j=J))
             sre_t[c] = sre
             sim = io.tile([P, J * WIDTH], BF16, tag="sim", name="sim")
-            nc.sync.dma_start(out=sim[:], in_=state_im[c * R:(c + 1) * R, :].rearrange("(i j) k -> i (j k)", j=J))
+            nc.sync.dma_start(out=sim[:], in_=rows_of(state_im, c).rearrange("(i j) k -> i (j k)", j=J))
             sim_t[c] = sim
 
-        def load_w(w, nm):
-            raw = const.tile([P, 4 * WIDTH], BF16, name="raw_" + nm)
+        def load_w(w, nm, tg):
+            raw = work.tile([P, 4 * WIDTH], BF16, tag=tg, name="raw_" + nm)
             nc.sync.dma_start(
                 out=raw[:].rearrange("p (u x) -> p u x", u=2),
                 in_=w.rearrange("(u q e) c -> q u (e c)", u=2, e=2),
             )
             return raw
 
+        raw_bre = load_w(B_re, "bre", "xore")
+        raw_bim = load_w(B_im, "bim", "xore")
         load_u(0)
-        raw_bre = load_w(B_re, "bre")
-        raw_bim = load_w(B_im, "bim")
         load_s(0)
-        raw_cre = load_w(C_re, "cre")
-        raw_cim = load_w(C_im, "cim")
         load_u(1)
+        raw_cre = load_w(C_re, "cre", "xoim")
+        raw_cim = load_w(C_im, "cim", "xoim")
         load_s(1)
         load_u(2)
         load_s(2)
+        load_u(3)
 
         ident = const.tile([P, P], F32, name="ident")
         make_identity(nc, ident[:])
@@ -89,14 +103,40 @@ def tile_linearrecurrentunitcell_t_kernel(
         def small(nm, dt=F32):
             return const.tile([P, 4], dt, name=nm)
 
-        e1 = small("e1")
-        nc.scalar.activation(out=e1[:], in_=pr_nu[:], func=ACTF.Exp)
-        mag = small("mag")
-        nc.scalar.activation(out=mag[:], in_=e1[:], func=ACTF.Exp, scale=-1.0)
+        def codes(nm):
+            cd = const.tile([P, WIDTH], U32, name="cd_" + nm, align_bytes=64)
+            sc = const.tile([P, WIDTH], U8, name="sc_" + nm, align_bytes=64)
+            return cd, sc
+
+        def quant(g, nm):
+            cd, sc = codes(nm)
+            nc.vector.quantize_mx(out=cd[:].bitcast(FP8X4), scales=sc[:], in_=g[:])
+            return cd, sc
+
+        def regroup_b(raw, nm, eng):
+            g = work.tile([P, 4 * WIDTH], BF16, tag="gxre", name="g_" + nm, align_bytes=64)
+            src = raw[:].rearrange("p (t u q e) -> p u e q t", t=4, u=2, e=2)
+            dst = g[:].rearrange("p (u e q t) -> p u e q t", u=2, e=2, t=4)
+            for uu in range(2):
+                if eng == "v":
+                    nc.vector.tensor_copy(out=dst[:, uu], in_=src[:, uu])
+                else:
+                    nc.gpsimd.tensor_scalar(
+                        out=dst[:, uu], in0=src[:, uu], scalar1=1.0, scalar2=0.0, op0=ALU.mult, op1=ALU.add
+                    )
+            return g
+
+        def regroup_c(raw, nm, sign):
+            g = work.tile([P, 4 * WIDTH], BF16, tag="gxim", name="g_" + nm, align_bytes=64)
+            nc.gpsimd.tensor_scalar(
+                out=g[:].rearrange("p (n t) -> p n t", t=4),
+                in0=raw[:].rearrange("p (t n) -> p n t", t=4),
+                scalar1=sign, scalar2=0.0, op0=ALU.mult, op1=ALU.add,
+            )
+            return g
+
         thf = small("thf")
         nc.vector.tensor_copy(out=thf[:], in_=pr_th[:])
-        gam = small("gam")
-        nc.vector.tensor_copy(out=gam[:], in_=pr_ga[:])
         kq = small("kq")
         nc.vector.tensor_scalar_mul(out=kq[:], in0=thf[:], scalar1=1.0 / (2.0 * math.pi))
         ki = small("ki", I32)
@@ -107,10 +147,22 @@ def tile_linearrecurrentunitcell_t_kernel(
         nc.vector.scalar_tensor_tensor(out=r1[:], in0=kf[:], scalar=-TWO_PI_HI, in1=thf[:], op0=ALU.mult, op1=ALU.add)
         r2 = small("r2")
         nc.vector.scalar_tensor_tensor(out=r2[:], in0=kf[:], scalar=-TWO_PI_LO, in1=r1[:], op0=ALU.mult, op1=ALU.add)
+        gam = small("gam")
+        nc.vector.tensor_copy(out=gam[:], in_=pr_ga[:])
+        e1 = small("e1")
+        nc.scalar.activation(out=e1[:], in_=pr_nu[:], func=ACTF.Exp)
+        mag = small("mag")
+        nc.scalar.activation(out=mag[:], in_=e1[:], func=ACTF.Exp, scale=-1.0)
         sa = small("sa")
         nc.scalar.activation(out=sa[:], in_=r2[:], func=ACTF.Sin, scale=0.5)
         sb = small("sb")
         nc.scalar.activation(out=sb[:], in_=r2[:], func=ACTF.Sin, scale=0.25)
+
+        g_bre = regroup_b(raw_bre, "bre", "v")
+        g_bim = regroup_b(raw_bim, "bim", "g")
+        g_cre = regroup_c(raw_cre, "cre", 1.0)
+        g_cim = regroup_c(raw_cim, "cim", -1.0)
+
         sa2 = small("sa2")
         nc.vector.tensor_tensor(out=sa2[:], in0=sa[:], in1=sa[:], op=ALU.mult)
         cosr = small("cosr")
@@ -128,96 +180,45 @@ def tile_linearrecurrentunitcell_t_kernel(
         nlam_im = small("nlam_im")
         nc.vector.tensor_scalar_mul(out=nlam_im[:], in0=lam_im[:], scalar1=-1.0)
 
-        def codes(nm):
-            cd = const.tile([P, WIDTH], U32, name="cd_" + nm, align_bytes=64)
-            sc = const.tile([P, WIDTH], U8, name="sc_" + nm, align_bytes=64)
-            return cd, sc
+        b_cd = [quant(g_bre, "bre"), quant(g_bim, "bim")]
+        c_cd = [None, None]
 
-        def prep_b(raw, nm):
-            g = work.tile([P, 4 * WIDTH], BF16, tag="gw", name="g_" + nm, align_bytes=64)
-            src = raw[:].rearrange("p (t u q e) -> p u e q t", t=4, u=2, e=2)
-            dst = g[:].rearrange("p (u e q t) -> p u e q t", u=2, e=2, t=4)
-            for uu in range(2):
-                nc.vector.tensor_copy(out=dst[:, uu], in_=src[:, uu])
-            cd, sc = codes(nm)
-            nc.vector.quantize_mx(out=cd[:].bitcast(FP8X4), scales=sc[:], in_=g[:])
-            return cd, sc
-
-        def prep_c(raw, nm, sign):
-            g = work.tile([P, 4 * WIDTH], BF16, tag="gw", name="g_" + nm, align_bytes=64)
-            nc.gpsimd.tensor_scalar(
-                out=g[:].rearrange("p (n t) -> p n t", t=4),
-                in0=raw[:].rearrange("p (t n) -> p n t", t=4),
-                scalar1=sign, scalar2=0.0, op0=ALU.mult, op1=ALU.add,
-            )
-            cd, sc = codes(nm)
-            nc.vector.quantize_mx(out=cd[:].bitcast(FP8X4), scales=sc[:], in_=g[:])
-            return cd, sc
-
-        b_cd = [prep_b(raw_bre, "bre"), prep_b(raw_bim, "bim")]
-        c_cd = [prep_c(raw_cre, "cre", 1.0), prep_c(raw_cim, "cim", -1.0)]
-
+        gu_t = {}
+        ut_t = {}
         uq_t = {}
         du_t = {}
         xT_t = {}
+        gx_t = {}
         xq_t = {}
         xo_t = {}
         yo_t = {}
-
-        def prep_u(c):
-            u_w = u_t[c][:].bitcast(F32)
-            gu = work.tile([P, 4 * R], BF16, tag="gu", name="gu", align_bytes=64)
-            gu_w = gu[:].bitcast(F32).rearrange("p (m u) -> p m u", u=2)
-            for hc in range(J // 2):
-                ut = psum.tile([P, 2, 256], F32, tag="ut", name="ut")
-                for jj in range(2):
-                    j = 2 * hc + jj
-                    for u in range(2):
-                        nc.tensor.transpose(
-                            ut[:, u, jj * P:(jj + 1) * P], u_w[:, j * 256 + u * P:j * 256 + (u + 1) * P], ident[:]
-                        )
-                nc.scalar.copy(out=gu_w[:, hc * 256:(hc + 1) * 256, :], in_=ut[:].rearrange("p u m -> p m u"))
-            uc = work.tile([P, R], U32, tag="uc", name="uc", align_bytes=64)
-            us = work.tile([P, R], U8, tag="us", name="us", align_bytes=64)
-            nc.vector.quantize_mx(out=uc[:].bitcast(FP8X4), scales=us[:], in_=gu[:])
-            uq_t[c] = (uc, us)
-
-        def skip_term(c):
-            du = work.tile([P, J, WIDTH], F32, tag="du", name="du")
-            nc.gpsimd.tensor_tensor(
-                out=du[:],
-                in0=u_t[c][:].rearrange("p (j k) -> p j k", j=J),
-                in1=dbc[:].unsqueeze(1).to_broadcast([P, J, WIDTH]),
-                op=ALU.mult,
-            )
-            du_t[c] = du
-
         st_t = {}
+        pp_t = {}
+        xn_t = {}
+        yy_t = {}
 
-        def main_step(c, t):
-            u, e = divmod(t, 2)
-            if t == 0:
-                xre = work.tile([P, 4, R], F32, tag="xTre", name="xTre")
-                xim = work.tile([P, 4, R], F32, tag="xTim", name="xTim")
-                xT_t[c] = (xre, xim)
-            xre, xim = xT_t[c]
-            if e == 0:
-                pair = []
-                for src_t, tg in ((sre_t[c], "str"), (sim_t[c], "sti")):
-                    s_w = src_t[:].bitcast(F32)
-                    st = psum.tile([P, R], F32, tag=tg, name=tg)
-                    for j in range(J):
-                        nc.tensor.transpose(
-                            st[:, j * P:(j + 1) * P], s_w[:, j * 256 + u * P:j * 256 + (u + 1) * P], ident[:]
-                        )
-                    pair.append(st[:].bitcast(BF16).rearrange("p (m e) -> p m e", e=2))
-                st_t[c] = pair
-            s_re, s_im = st_t[c]
-            col = slice(t, t + 1)
-            nc.scalar.activation(out=xre[:, t, :], in_=s_re[:, :, e], func=ACTF.Copy, scale=lam_re[:, col])
-            nc.scalar.activation(out=xim[:, t, :], in_=s_re[:, :, e], func=ACTF.Copy, scale=lam_im[:, col])
+        def pe_ut(c, hc):
+            u_w = u_t[c][:].bitcast(F32)
+            ut = psum.tile([P, 2, 256], F32, tag="ut", name="ut")
+            for jj in range(2):
+                j = 2 * hc + jj
+                for u in range(2):
+                    nc.tensor.transpose(
+                        ut[:, u, jj * P:(jj + 1) * P], u_w[:, j * 256 + u * P:j * 256 + (u + 1) * P], ident[:]
+                    )
+            ut_t[(c, hc)] = ut
+
+        def pe_st(c, u, which):
+            src_t, tg = ((sre_t, "str"), (sim_t, "sti"))[which]
+            s_w = src_t[c][:].bitcast(F32)
+            st = psum.tile([P, R], F32, tag=tg, name=tg)
+            for j in range(J):
+                nc.tensor.transpose(st[:, j * P:(j + 1) * P], s_w[:, j * 256 + u * P:j * 256 + (u + 1) * P], ident[:])
+            st_t[(c, u, which)] = st[:].bitcast(BF16).rearrange("p (m e) -> p m e", e=2)
+
+        def pe_m1(g):
+            c, t = divmod(g, 4)
             uc, us = uq_t[c]
-            pps = []
             for ri in range(2):
                 cd, sc = b_cd[ri]
                 pp = psum.tile([P, R], F32, tag="pp", name="pp", bufs=2)
@@ -227,63 +228,27 @@ def tile_linearrecurrentunitcell_t_kernel(
                     rhs=uc[:].bitcast(FP8X4), rhs_scale=us[:],
                     start=True, stop=True,
                 )
-                pps.append(pp)
-            nc.vector.scalar_tensor_tensor(
-                out=xre[:, t, :], in0=s_im[:, :, e], scalar=nlam_im[:, col], in1=xre[:, t, :], op0=ALU.mult, op1=ALU.add
-            )
-            nc.vector.scalar_tensor_tensor(
-                out=xim[:, t, :], in0=s_im[:, :, e], scalar=lam_re[:, col], in1=xim[:, t, :], op0=ALU.mult, op1=ALU.add
-            )
-            nc.vector.scalar_tensor_tensor(
-                out=xre[:, t, :], in0=pps[0][:], scalar=gam[:, col], in1=xre[:, t, :], op0=ALU.mult, op1=ALU.add
-            )
-            nc.vector.scalar_tensor_tensor(
-                out=xim[:, t, :], in0=pps[1][:], scalar=gam[:, col], in1=xim[:, t, :], op0=ALU.mult, op1=ALU.add
-            )
+                pp_t[(g, ri)] = pp
 
-        gx_t = {}
-
-        def cast_x(c):
-            gs = []
-            for ri, tg in ((0, "gxre"), (1, "gxim")):
-                gx = work.tile([P, 4 * R], BF16, tag=tg, name=tg, align_bytes=64)
-                nc.gpsimd.tensor_scalar(
-                    out=gx[:].rearrange("p (m t) -> p m t", t=4),
-                    in0=xT_t[c][ri][:].rearrange("p t m -> p m t"),
-                    scalar1=1.0, scalar2=0.0, op0=ALU.mult, op1=ALU.add,
-                )
-                gs.append(gx)
-            gx_t[c] = gs
-
-        def quant_x(c):
-            qs = []
-            for ri, tg in ((0, "re"), (1, "im")):
-                xc = work.tile([P, R], U32, tag="xc" + tg, name="xc" + tg, align_bytes=64)
-                xs = work.tile([P, R], U8, tag="xs" + tg, name="xs" + tg, align_bytes=64)
-                nc.vector.quantize_mx(out=xc[:].bitcast(FP8X4), scales=xs[:], in_=gx_t[c][ri][:])
-                qs.append((xc, xs))
-            xq_t[c] = qs
-
-        def xback(c, j):
-            if j == 0:
-                xore = work.tile([P, J, WIDTH], F32, tag="xore", name="xore")
-                xoim = work.tile([P, J, WIDTH], F32, tag="xoim", name="xoim")
-                xo_t[c] = (xore, xoim)
+        def pe_xb(q):
+            c, r = divmod(q, 4)
+            u, jp = divmod(r, 2)
             for ri in range(2):
-                xn = psum.tile([P, WIDTH], F32, tag="xn", name="xn", bufs=2)
-                for t in range(4):
-                    nc.tensor.transpose(xn[:, t * P:(t + 1) * P], xT_t[c][ri][:, t, j * P:(j + 1) * P], ident[:])
-                nc.scalar.copy(
-                    out=xo_t[c][ri][:, j, :].rearrange("p (u q e) -> p u q e", u=2, e=2),
-                    in_=xn[:].rearrange("p (u e q) -> p u q e", u=2, e=2),
-                )
+                xn = psum.tile([P, 2, 2, P], F32, tag="xn", name="xn", bufs=2)
+                for jj in range(2):
+                    j = 2 * jp + jj
+                    for e in range(2):
+                        nc.tensor.transpose(xn[:, jj, e, :], xT_t[c][ri][:, 2 * u + e, j * P:(j + 1) * P], ident[:])
+                xn_t[(q, ri)] = xn
 
-        def ystep(c, j):
-            if j == 0:
-                yo_t[c] = work.tile([P, J, WIDTH], F32, tag="yo", name="yo")
-            yy = psum.tile([P, WIDTH], F32, tag="yy", name="yy")
+        def pe_m2(yi):
+            c, j = divmod(yi, 4)
+            tg = "yy"
+            if yi >= NPL - 7 and yi % 3 != 0:
+                tg = "pp"
+            yy = psum.tile([P, WIDTH], F32, tag=tg, name="yy", bufs=(1 if tg == "yy" else 2))
             for ri in range(2):
-                xc, xs = xq_t[c][ri]
+                xc, xs = xq_t[(c, ri)]
                 cd, sc = c_cd[ri]
                 nc.tensor.matmul_mx(
                     out=yy[:],
@@ -291,34 +256,159 @@ def tile_linearrecurrentunitcell_t_kernel(
                     rhs=cd[:].bitcast(FP8X4), rhs_scale=sc[:],
                     start=(ri == 0), stop=(ri == 1),
                 )
-            nc.vector.tensor_tensor(out=yo_t[c][:, j, :], in0=yy[:], in1=du_t[c][:, j, :], op=ALU.add)
+            yy_t[yi] = yy
 
-        def store(dst, c, src):
-            nc.sync.dma_start(out=dst[c * R:(c + 1) * R, :].rearrange("(i j) h -> i j h", j=J), in_=src[:])
+        def act_ut(c, hc):
+            if hc == 0:
+                gu_t[c] = work.tile([P, 4 * R], BF16, tag="gu", name="gu", align_bytes=64)
+            gu_w = gu_t[c][:].bitcast(F32).rearrange("p (m u) -> p m u", u=2)
+            nc.scalar.copy(out=gu_w[:, hc * 256:(hc + 1) * 256, :], in_=ut_t[(c, hc)][:].rearrange("p u m -> p m u"))
 
-        prep_u(0)
-        for c in range(NCH + 1):
-            prev = c - 1
-            if prev >= 0:
-                cast_x(prev)
-            if c < NCH:
-                skip_term(c)
-            if c + 1 < NCH:
-                prep_u(c + 1)
-            for k in range(4):
-                if c < NCH:
-                    main_step(c, k)
-                if prev >= 0:
-                    xback(prev, k)
-                    if k == 1:
-                        quant_x(prev)
-                    if k >= 2:
-                        ystep(prev, 2 * (k - 2))
-                        ystep(prev, 2 * (k - 2) + 1)
-            if prev >= 0:
-                store(out_1, prev, xo_t[prev][0])
-                store(out_2, prev, xo_t[prev][1])
-                store(out_0, prev, yo_t[prev])
-            if c + 3 < NCH:
-                load_u(c + 3)
+        def act_a(g):
+            c, t = divmod(g, 4)
+            u, e = divmod(t, 2)
+            if t == 0:
+                xre = work.tile([P, 4, R], F32, tag="xTre", name="xTre", bufs=3)
+                xim = work.tile([P, 4, R], F32, tag="xTim", name="xTim", bufs=3)
+                xT_t[c] = (xre, xim)
+            xre, xim = xT_t[c]
+            s_re = st_t[(c, u, 0)]
+            nc.scalar.activation(out=xre[:, t, :], in_=s_re[:, :, e], func=ACTF.Copy, scale=lam_re[:, t:t + 1])
+            nc.scalar.activation(out=xim[:, t, :], in_=s_re[:, :, e], func=ACTF.Copy, scale=lam_im[:, t:t + 1])
+
+        def act_xn(q):
+            c, r = divmod(q, 4)
+            u, jp = divmod(r, 2)
+            if r == 0:
+                xore = work.tile([P, J, WIDTH], F32, tag="xore", name="xore")
+                xoim = work.tile([P, J, WIDTH], F32, tag="xoim", name="xoim")
+                xo_t[c] = (xore, xoim)
+            for ri in range(2):
+                nc.scalar.copy(
+                    out=xo_t[c][ri][:, 2 * jp:2 * jp + 2, 256 * u:256 * u + 256].rearrange("p j (q e) -> p j q e", e=2),
+                    in_=xn_t[(q, ri)][:].rearrange("p j e q -> p j q e"),
+                )
+
+        def dve_b(g):
+            c, t = divmod(g, 4)
+            u, e = divmod(t, 2)
+            xre, xim = xT_t[c]
+            s_im = st_t[(c, u, 1)]
+            nc.vector.scalar_tensor_tensor(
+                out=xre[:, t, :], in0=s_im[:, :, e], scalar=nlam_im[:, t:t + 1], in1=xre[:, t, :],
+                op0=ALU.mult, op1=ALU.add,
+            )
+            nc.vector.scalar_tensor_tensor(
+                out=xim[:, t, :], in0=s_im[:, :, e], scalar=lam_re[:, t:t + 1], in1=xim[:, t, :],
+                op0=ALU.mult, op1=ALU.add,
+            )
+
+        def dve_x(g):
+            c, t = divmod(g, 4)
+            for ri in range(2):
+                x = xT_t[c][ri]
+                nc.vector.scalar_tensor_tensor(
+                    out=x[:, t, :], in0=pp_t[(g, ri)][:], scalar=gam[:, t:t + 1], in1=x[:, t, :],
+                    op0=ALU.mult, op1=ALU.add,
+                )
+
+        def dve_qu(c):
+            uc = work.tile([P, R], U32, tag="uc", name="uc", align_bytes=64)
+            us = work.tile([P, R], U8, tag="us", name="us", align_bytes=64)
+            nc.vector.quantize_mx(out=uc[:].bitcast(FP8X4), scales=us[:], in_=gu_t[c][:])
+            uq_t[c] = (uc, us)
+
+        def dve_qx(c, ri):
+            tg = ("re", "im")[ri]
+            xc = work.tile([P, R], U32, tag="xc" + tg, name="xc" + tg, align_bytes=64)
+            xs = work.tile([P, R], U8, tag="xs" + tg, name="xs" + tg, align_bytes=64)
+            nc.vector.quantize_mx(out=xc[:].bitcast(FP8X4), scales=xs[:], in_=gx_t[(c, ri)][:])
+            xq_t[(c, ri)] = (xc, xs)
+
+        def dve_y(yi):
+            c, j = divmod(yi, 4)
+            if j == 0:
+                yo_t[c] = work.tile([P, J, WIDTH], F32, tag="yo", name="yo")
+            nc.vector.tensor_tensor(
+                out=yo_t[c][:, j, :], in0=yy_t[yi][:], in1=du_t[(c, j // 2)][:, j % 2, :], op=ALU.add
+            )
+
+        def pool_du(c, h):
+            du = work.tile([P, 2, WIDTH], F32, tag="du", name="du", bufs=4)
+            nc.gpsimd.tensor_tensor(
+                out=du[:],
+                in0=u_t[c][:, 2 * h * WIDTH:(2 * h + 2) * WIDTH].rearrange("p (j k) -> p j k", j=2),
+                in1=dbc[:].unsqueeze(1).to_broadcast([P, 2, WIDTH]),
+                op=ALU.mult,
+            )
+            du_t[(c, h)] = du
+
+        def cast_x(c, ri, eng):
+            tg = ("gxre", "gxim")[ri]
+            gx = work.tile([P, 4 * R], BF16, tag=tg, name=tg, align_bytes=64)
+            dst = gx[:].rearrange("p (m t) -> p m t", t=4)
+            src = xT_t[c][ri][:].rearrange("p t m -> p m t")
+            if eng == "v":
+                nc.vector.tensor_copy(out=dst, in_=src)
+            else:
+                nc.gpsimd.tensor_scalar(out=dst, in0=src, scalar1=1.0, scalar2=0.0, op0=ALU.mult, op1=ALU.add)
+            gx_t[(c, ri)] = gx
+
+        def store(dram, c, src, j0, j1):
+            nc.sync.dma_start(
+                out=rows_of(dram, c).rearrange("(i j) h -> i j h", j=J)[:, j0:j1, :], in_=src[:, j0:j1, :]
+            )
+
+        for g in range(-8, NPL + 7):
+            c, k = divmod(g, 4)
+            if okp(g):
+                dve_x(g)
+            if k == 0 and ok(c + 1):
+                dve_qu(c + 1)
+            if k in (1, 2):
+                if ok(c - 1):
+                    dve_qx(c - 1, k - 1)
+                elif c == 0:
+                    c_cd[k - 1] = quant((g_cre, g_cim)[k - 1], ("cre", "cim")[k - 1])
+            if okp(g - 7):
+                dve_y(g - 7)
+            if okp(g + 2):
+                act_a(g + 2)
+            if okp(g - 2):
+                act_xn(g - 2)
+            if k in (1, 3) and ok(c + 2):
+                act_ut(c + 2, (k - 1) // 2)
+            if k in (0, 2) and ok(c):
+                pool_du(c, k // 2)
+            if k == 3 and ok(c):
+                cast_x(c, 0, "g")
+                cast_x(c, 1, "v" if c == NCH - 1 else "g")
+            if k == 2 and ok(c + 3):
                 load_s(c + 3)
+            if k == 3 and ok(c + 4):
+                load_u(c + 4)
+            if k == 1 and ok(c - 1):
+                store(out_1, c - 1, xo_t[c - 1][0], 0, J)
+                store(out_2, c - 1, xo_t[c - 1][1], 0, J)
+            if k == 2 and ok(c - 2):
+                if c - 2 == NCH - 1:
+                    store(out_0, c - 2, yo_t[c - 2], 2, J)
+                else:
+                    store(out_0, c - 2, yo_t[c - 2], 0, J)
+            if k == 0 and c - 2 == NCH - 1:
+                store(out_0, c - 2, yo_t[c - 2], 0, 2)
+            if okp(g + 1):
+                pe_m1(g + 1)
+            c1, k1 = divmod(g + 1, 4)
+            if k1 in (1, 3) and ok(c1 + 2):
+                pe_ut(c1 + 2, (k1 - 1) // 2)
+            if okp(g + 1) and (g + 1) % 2 == 0:
+                pe_st((g + 1) // 4, ((g + 1) % 4) // 2, 1)
+            if okp(g + 3) and (g + 3) % 2 == 0:
+                pe_st((g + 3) // 4, ((g + 3) % 4) // 2, 0)
+            if okp(g - 1):
+                pe_xb(g - 1)
+            if okp(g - 6):
+                pe_m2(g - 6)
+            if okp(g + 1):
+                dve_b(g + 1)

@@ -16,15 +16,18 @@ ACTF = mybir.ActivationFunctionType
 P = 128
 ROWS = 4096
 WIDTH = 512
-R = 512
-J = R // P
-NCH = ROWS // R
-NPL = 4 * NCH
 FLOPS = 4 * 2 * ROWS * WIDTH * WIDTH
 
 TWO_PI_HI = 6.28125
 TWO_PI_LO = 2.0 * math.pi - 6.28125
-PIN = True
+CHUNKS = [512] * 7 + [256, 256]
+
+NCH = len(CHUNKS)
+NPL = 4 * NCH
+OFFS = [sum(CHUNKS[:c]) for c in range(NCH)]
+assert sum(CHUNKS) == ROWS
+YLAG = 7
+KQ = 2
 
 
 def tile_linearrecurrentunitcell_t_kernel(
@@ -32,8 +35,7 @@ def tile_linearrecurrentunitcell_t_kernel(
 ):
     nc = tc.nc
     with ExitStack() as ctx:
-        if PIN:
-            ctx.enter_context(tc.manual_schedule())
+        ctx.enter_context(tc.manual_schedule())
         const = ctx.enter_context(tc.tile_pool(name="const", bufs=1))
         io = ctx.enter_context(tc.tile_pool(name="io", bufs=3))
         work = ctx.enter_context(tc.tile_pool(name="work", bufs=2))
@@ -44,6 +46,12 @@ def tile_linearrecurrentunitcell_t_kernel(
 
         def okp(g):
             return 0 <= g < NPL
+
+        def rows(c):
+            return CHUNKS[c]
+
+        def mt(c):
+            return CHUNKS[c] // P
 
         pr_nu = const.tile([P, 4], BF16, name="pr_nu")
         pr_th = const.tile([P, 4], BF16, name="pr_th")
@@ -62,19 +70,19 @@ def tile_linearrecurrentunitcell_t_kernel(
         sim_t = {}
 
         def rows_of(dram, c):
-            return dram[c * R:(c + 1) * R, :]
+            return dram[OFFS[c]:OFFS[c] + rows(c), :]
 
         def load_u(c):
-            u_sb = io.tile([P, J * WIDTH], BF16, tag="u", name="u_sb", bufs=4)
-            nc.sync.dma_start(out=u_sb[:], in_=rows_of(inputs, c).rearrange("(i j) k -> i (j k)", j=J))
+            u_sb = io.tile([P, mt(c) * WIDTH], BF16, tag="u", name="u_sb", bufs=4)
+            nc.sync.dma_start(out=u_sb[:], in_=rows_of(inputs, c).rearrange("(i j) k -> i (j k)", j=mt(c)))
             u_t[c] = u_sb
 
         def load_s(c):
-            sre = io.tile([P, J * WIDTH], BF16, tag="sre", name="sre")
-            nc.sync.dma_start(out=sre[:], in_=rows_of(state_re, c).rearrange("(i j) k -> i (j k)", j=J))
+            sre = io.tile([P, mt(c) * WIDTH], BF16, tag="sre", name="sre")
+            nc.sync.dma_start(out=sre[:], in_=rows_of(state_re, c).rearrange("(i j) k -> i (j k)", j=mt(c)))
             sre_t[c] = sre
-            sim = io.tile([P, J * WIDTH], BF16, tag="sim", name="sim")
-            nc.sync.dma_start(out=sim[:], in_=rows_of(state_im, c).rearrange("(i j) k -> i (j k)", j=J))
+            sim = io.tile([P, mt(c) * WIDTH], BF16, tag="sim", name="sim")
+            nc.sync.dma_start(out=sim[:], in_=rows_of(state_im, c).rearrange("(i j) k -> i (j k)", j=mt(c)))
             sim_t[c] = sim
 
         def load_w(w, nm, tg):
@@ -103,36 +111,18 @@ def tile_linearrecurrentunitcell_t_kernel(
         def small(nm, dt=F32):
             return const.tile([P, 4], dt, name=nm)
 
-        def codes(nm):
+        def quant(g_ap, nm):
             cd = const.tile([P, WIDTH], U32, name="cd_" + nm, align_bytes=64)
             sc = const.tile([P, WIDTH], U8, name="sc_" + nm, align_bytes=64)
+            nc.vector.quantize_mx(out=cd[:].bitcast(FP8X4), scales=sc[:], in_=g_ap)
             return cd, sc
 
-        def quant(g, nm):
-            cd, sc = codes(nm)
-            nc.vector.quantize_mx(out=cd[:].bitcast(FP8X4), scales=sc[:], in_=g[:])
-            return cd, sc
-
-        def regroup_b(raw, nm, eng):
+        def regroup_b(raw, nm):
             g = work.tile([P, 4 * WIDTH], BF16, tag="gxre", name="g_" + nm, align_bytes=64)
             src = raw[:].rearrange("p (t u q e) -> p u e q t", t=4, u=2, e=2)
             dst = g[:].rearrange("p (u e q t) -> p u e q t", u=2, e=2, t=4)
             for uu in range(2):
-                if eng == "v":
-                    nc.vector.tensor_copy(out=dst[:, uu], in_=src[:, uu])
-                else:
-                    nc.gpsimd.tensor_scalar(
-                        out=dst[:, uu], in0=src[:, uu], scalar1=1.0, scalar2=0.0, op0=ALU.mult, op1=ALU.add
-                    )
-            return g
-
-        def regroup_c(raw, nm, sign):
-            g = work.tile([P, 4 * WIDTH], BF16, tag="gxim", name="g_" + nm, align_bytes=64)
-            nc.gpsimd.tensor_scalar(
-                out=g[:].rearrange("p (n t) -> p n t", t=4),
-                in0=raw[:].rearrange("p (t n) -> p n t", t=4),
-                scalar1=sign, scalar2=0.0, op0=ALU.mult, op1=ALU.add,
-            )
+                nc.vector.tensor_copy(out=dst[:, uu], in_=src[:, uu])
             return g
 
         thf = small("thf")
@@ -158,10 +148,8 @@ def tile_linearrecurrentunitcell_t_kernel(
         sb = small("sb")
         nc.scalar.activation(out=sb[:], in_=r2[:], func=ACTF.Sin, scale=0.25)
 
-        g_bre = regroup_b(raw_bre, "bre", "v")
-        g_bim = regroup_b(raw_bim, "bim", "g")
-        g_cre = regroup_c(raw_cre, "cre", 1.0)
-        g_cim = regroup_c(raw_cim, "cim", -1.0)
+        g_bre = regroup_b(raw_bre, "bre")
+        g_bim = regroup_b(raw_bim, "bim")
 
         sa2 = small("sa2")
         nc.vector.tensor_tensor(out=sa2[:], in0=sa[:], in1=sa[:], op=ALU.mult)
@@ -180,8 +168,8 @@ def tile_linearrecurrentunitcell_t_kernel(
         nlam_im = small("nlam_im")
         nc.vector.tensor_scalar_mul(out=nlam_im[:], in0=lam_im[:], scalar1=-1.0)
 
-        b_cd = [quant(g_bre, "bre"), quant(g_bim, "bim")]
-        c_cd = [None, None]
+        b_cd = [quant(g_bre[:], "bre"), quant(g_bim[:], "bim")]
+        c_cd = []
 
         gu_t = {}
         ut_t = {}
@@ -197,6 +185,15 @@ def tile_linearrecurrentunitcell_t_kernel(
         xn_t = {}
         yy_t = {}
 
+        gu_t[1] = work.tile([P, 4 * rows(1)], BF16, tag="du", name="gu1", align_bytes=64)
+        g_c = work.tile([P, 2, 4 * WIDTH], BF16, tag="du", name="g_c", align_bytes=64)
+        for ri, (raw, sign) in enumerate(((raw_cre, 1.0), (raw_cim, -1.0))):
+            nc.gpsimd.tensor_scalar(
+                out=g_c[:, ri, :].rearrange("p (n t) -> p n t", t=4),
+                in0=raw[:].rearrange("p (t n) -> p n t", t=4),
+                scalar1=sign, scalar2=0.0, op0=ALU.mult, op1=ALU.add,
+            )
+
         def pe_ut(c, hc):
             u_w = u_t[c][:].bitcast(F32)
             ut = psum.tile([P, 2, 256], F32, tag="ut", name="ut")
@@ -211,8 +208,8 @@ def tile_linearrecurrentunitcell_t_kernel(
         def pe_st(c, u, which):
             src_t, tg = ((sre_t, "str"), (sim_t, "sti"))[which]
             s_w = src_t[c][:].bitcast(F32)
-            st = psum.tile([P, R], F32, tag=tg, name=tg)
-            for j in range(J):
+            st = psum.tile([P, rows(c)], F32, tag=tg, name=tg)
+            for j in range(mt(c)):
                 nc.tensor.transpose(st[:, j * P:(j + 1) * P], s_w[:, j * 256 + u * P:j * 256 + (u + 1) * P], ident[:])
             st_t[(c, u, which)] = st[:].bitcast(BF16).rearrange("p (m e) -> p m e", e=2)
 
@@ -221,7 +218,7 @@ def tile_linearrecurrentunitcell_t_kernel(
             uc, us = uq_t[c]
             for ri in range(2):
                 cd, sc = b_cd[ri]
-                pp = psum.tile([P, R], F32, tag="pp", name="pp", bufs=2)
+                pp = psum.tile([P, rows(c)], F32, tag="pp", name="pp", bufs=2)
                 nc.tensor.matmul_mx(
                     out=pp[:],
                     lhsT=cd[:, t * P:(t + 1) * P].bitcast(FP8X4), lhsT_scale=sc[:, t * P:(t + 1) * P],
@@ -233,6 +230,8 @@ def tile_linearrecurrentunitcell_t_kernel(
         def pe_xb(q):
             c, r = divmod(q, 4)
             u, jp = divmod(r, 2)
+            if 2 * jp >= mt(c):
+                return
             for ri in range(2):
                 xn = psum.tile([P, 2, 2, P], F32, tag="xn", name="xn", bufs=2)
                 for jj in range(2):
@@ -241,11 +240,11 @@ def tile_linearrecurrentunitcell_t_kernel(
                         nc.tensor.transpose(xn[:, jj, e, :], xT_t[c][ri][:, 2 * u + e, j * P:(j + 1) * P], ident[:])
                 xn_t[(q, ri)] = xn
 
-        def pe_m2(yi):
+        def pe_m2(yi, spare_banks):
             c, j = divmod(yi, 4)
-            tg = "yy"
-            if yi >= NPL - 7 and yi % 3 != 0:
-                tg = "pp"
+            if j >= mt(c):
+                return
+            tg = "pp" if (spare_banks and yi % 3 != 0) else "yy"
             yy = psum.tile([P, WIDTH], F32, tag=tg, name="yy", bufs=(1 if tg == "yy" else 2))
             for ri in range(2):
                 xc, xs = xq_t[(c, ri)]
@@ -259,8 +258,8 @@ def tile_linearrecurrentunitcell_t_kernel(
             yy_t[yi] = yy
 
         def act_ut(c, hc):
-            if hc == 0:
-                gu_t[c] = work.tile([P, 4 * R], BF16, tag="gu", name="gu", align_bytes=64)
+            if c not in gu_t:
+                gu_t[c] = work.tile([P, 4 * rows(c)], BF16, tag="gu", name="gu", align_bytes=64)
             gu_w = gu_t[c][:].bitcast(F32).rearrange("p (m u) -> p m u", u=2)
             nc.scalar.copy(out=gu_w[:, hc * 256:(hc + 1) * 256, :], in_=ut_t[(c, hc)][:].rearrange("p u m -> p m u"))
 
@@ -268,8 +267,8 @@ def tile_linearrecurrentunitcell_t_kernel(
             c, t = divmod(g, 4)
             u, e = divmod(t, 2)
             if t == 0:
-                xre = work.tile([P, 4, R], F32, tag="xTre", name="xTre", bufs=3)
-                xim = work.tile([P, 4, R], F32, tag="xTim", name="xTim", bufs=3)
+                xre = work.tile([P, 4, rows(c)], F32, tag="xTre", name="xTre", bufs=3)
+                xim = work.tile([P, 4, rows(c)], F32, tag="xTim", name="xTim", bufs=3)
                 xT_t[c] = (xre, xim)
             xre, xim = xT_t[c]
             s_re = st_t[(c, u, 0)]
@@ -280,9 +279,11 @@ def tile_linearrecurrentunitcell_t_kernel(
             c, r = divmod(q, 4)
             u, jp = divmod(r, 2)
             if r == 0:
-                xore = work.tile([P, J, WIDTH], F32, tag="xore", name="xore")
-                xoim = work.tile([P, J, WIDTH], F32, tag="xoim", name="xoim")
+                xore = work.tile([P, mt(c), WIDTH], F32, tag="xore", name="xore")
+                xoim = work.tile([P, mt(c), WIDTH], F32, tag="xoim", name="xoim")
                 xo_t[c] = (xore, xoim)
+            if 2 * jp >= mt(c):
+                return
             for ri in range(2):
                 nc.scalar.copy(
                     out=xo_t[c][ri][:, 2 * jp:2 * jp + 2, 256 * u:256 * u + 256].rearrange("p j (q e) -> p j q e", e=2),
@@ -313,102 +314,112 @@ def tile_linearrecurrentunitcell_t_kernel(
                 )
 
         def dve_qu(c):
-            uc = work.tile([P, R], U32, tag="uc", name="uc", align_bytes=64)
-            us = work.tile([P, R], U8, tag="us", name="us", align_bytes=64)
+            uc = work.tile([P, rows(c)], U32, tag="uc", name="uc", align_bytes=64)
+            us = work.tile([P, rows(c)], U8, tag="us", name="us", align_bytes=64)
             nc.vector.quantize_mx(out=uc[:].bitcast(FP8X4), scales=us[:], in_=gu_t[c][:])
             uq_t[c] = (uc, us)
 
         def dve_qx(c, ri):
             tg = ("re", "im")[ri]
-            xc = work.tile([P, R], U32, tag="xc" + tg, name="xc" + tg, align_bytes=64)
-            xs = work.tile([P, R], U8, tag="xs" + tg, name="xs" + tg, align_bytes=64)
+            xc = work.tile([P, rows(c)], U32, tag="xc" + tg, name="xc" + tg, align_bytes=64)
+            xs = work.tile([P, rows(c)], U8, tag="xs" + tg, name="xs" + tg, align_bytes=64)
             nc.vector.quantize_mx(out=xc[:].bitcast(FP8X4), scales=xs[:], in_=gx_t[(c, ri)][:])
             xq_t[(c, ri)] = (xc, xs)
 
         def dve_y(yi):
             c, j = divmod(yi, 4)
+            if j >= mt(c):
+                return
             if j == 0:
-                yo_t[c] = work.tile([P, J, WIDTH], F32, tag="yo", name="yo")
-            nc.vector.tensor_tensor(
-                out=yo_t[c][:, j, :], in0=yy_t[yi][:], in1=du_t[(c, j // 2)][:, j % 2, :], op=ALU.add
-            )
+                yo_t[c] = work.tile([P, mt(c), WIDTH], F32, tag="yo", name="yo")
+            nc.vector.tensor_tensor(out=yo_t[c][:, j, :], in0=yy_t[yi][:], in1=du_t[c][:, j, :], op=ALU.add)
+            if j == mt(c) - 1:
+                store(out_0, c, yo_t[c])
 
-        def pool_du(c, h):
-            du = work.tile([P, 2, WIDTH], F32, tag="du", name="du", bufs=4)
+        def pool_du(c):
+            du = work.tile([P, mt(c), WIDTH], F32, tag="du", name="du", align_bytes=64)
             nc.gpsimd.tensor_tensor(
                 out=du[:],
-                in0=u_t[c][:, 2 * h * WIDTH:(2 * h + 2) * WIDTH].rearrange("p (j k) -> p j k", j=2),
-                in1=dbc[:].unsqueeze(1).to_broadcast([P, 2, WIDTH]),
+                in0=u_t[c][:].rearrange("p (j k) -> p j k", j=mt(c)),
+                in1=dbc[:].unsqueeze(1).to_broadcast([P, mt(c), WIDTH]),
                 op=ALU.mult,
             )
-            du_t[(c, h)] = du
+            du_t[c] = du
 
         def cast_x(c, ri, eng):
             tg = ("gxre", "gxim")[ri]
-            gx = work.tile([P, 4 * R], BF16, tag=tg, name=tg, align_bytes=64)
+            gx = work.tile([P, 4 * rows(c)], BF16, tag=tg, name=tg, align_bytes=64)
             dst = gx[:].rearrange("p (m t) -> p m t", t=4)
             src = xT_t[c][ri][:].rearrange("p t m -> p m t")
-            if eng == "v":
-                nc.vector.tensor_copy(out=dst, in_=src)
+            if eng == "a":
+                nc.scalar.copy(out=dst, in_=src)
             else:
                 nc.gpsimd.tensor_scalar(out=dst, in0=src, scalar1=1.0, scalar2=0.0, op0=ALU.mult, op1=ALU.add)
             gx_t[(c, ri)] = gx
 
-        def store(dram, c, src, j0, j1):
-            nc.sync.dma_start(
-                out=rows_of(dram, c).rearrange("(i j) h -> i j h", j=J)[:, j0:j1, :], in_=src[:, j0:j1, :]
-            )
+        def store(dram, c, src):
+            nc.sync.dma_start(out=rows_of(dram, c).rearrange("(i j) h -> i j h", j=mt(c)), in_=src[:])
 
-        for g in range(-8, NPL + 7):
+        def ut_at(g):
+            c, k = divmod(g, 4)
+            w = None
+            if g in (-7, -5):
+                w = (0, (g + 7) // 2)
+            elif g in (0, 1):
+                w = (1, g)
+            elif c >= 0 and k >= 2 and ok(c + 2):
+                w = (c + 2, k - 2)
+            if w is not None and 2 * w[1] >= mt(w[0]):
+                w = None
+            return w
+
+        for g in range(-8, NPL + YLAG):
             c, k = divmod(g, 4)
             if okp(g):
                 dve_x(g)
-            if k == 0 and ok(c + 1):
-                dve_qu(c + 1)
-            if k in (1, 2):
+            if g == -4:
+                dve_qu(0)
+            if k == KQ:
                 if ok(c - 1):
-                    dve_qx(c - 1, k - 1)
-                elif c == 0:
-                    c_cd[k - 1] = quant((g_cre, g_cim)[k - 1], ("cre", "cim")[k - 1])
-            if okp(g - 7):
-                dve_y(g - 7)
+                    dve_qx(c - 1, 0)
+                    dve_qx(c - 1, 1)
+                if c == 1:
+                    c_cd.append(quant(g_c[:, 0, :], "cre"))
+                    c_cd.append(quant(g_c[:, 1, :], "cim"))
+                if c >= 0 and ok(c + 1):
+                    dve_qu(c + 1)
+            if okp(g - YLAG):
+                dve_y(g - YLAG)
             if okp(g + 2):
                 act_a(g + 2)
-            if okp(g - 2):
-                act_xn(g - 2)
-            if k in (1, 3) and ok(c + 2):
-                act_ut(c + 2, (k - 1) // 2)
-            if k in (0, 2) and ok(c):
-                pool_du(c, k // 2)
+            if k == KQ and ok(c):
+                pool_du(c)
             if k == 3 and ok(c):
                 cast_x(c, 0, "g")
-                cast_x(c, 1, "v" if c == NCH - 1 else "g")
-            if k == 2 and ok(c + 3):
-                load_s(c + 3)
-            if k == 3 and ok(c + 4):
-                load_u(c + 4)
+                cast_x(c, 1, "a" if c == NCH - 1 else "g")
+            if okp(g - 2):
+                act_xn(g - 2)
+            if ut_at(g) is not None:
+                act_ut(ut_at(g)[0], ut_at(g)[1])
+            if k == 2 and c >= 0:
+                if ok(c + 3):
+                    load_s(c + 3)
+                if ok(c + 4):
+                    load_u(c + 4)
             if k == 1 and ok(c - 1):
-                store(out_1, c - 1, xo_t[c - 1][0], 0, J)
-                store(out_2, c - 1, xo_t[c - 1][1], 0, J)
-            if k == 2 and ok(c - 2):
-                if c - 2 == NCH - 1:
-                    store(out_0, c - 2, yo_t[c - 2], 2, J)
-                else:
-                    store(out_0, c - 2, yo_t[c - 2], 0, J)
-            if k == 0 and c - 2 == NCH - 1:
-                store(out_0, c - 2, yo_t[c - 2], 0, 2)
-            if okp(g + 1):
-                pe_m1(g + 1)
-            c1, k1 = divmod(g + 1, 4)
-            if k1 in (1, 3) and ok(c1 + 2):
-                pe_ut(c1 + 2, (k1 - 1) // 2)
+                store(out_1, c - 1, xo_t[c - 1][0])
+                store(out_2, c - 1, xo_t[c - 1][1])
             if okp(g + 1) and (g + 1) % 2 == 0:
                 pe_st((g + 1) // 4, ((g + 1) % 4) // 2, 1)
+            if okp(g + 1):
+                pe_m1(g + 1)
+            if okp(g + 1 - YLAG):
+                pe_m2(g + 1 - YLAG, g >= NPL - 1)
+            if ut_at(g + 1) is not None:
+                pe_ut(ut_at(g + 1)[0], ut_at(g + 1)[1])
             if okp(g + 3) and (g + 3) % 2 == 0:
                 pe_st((g + 3) // 4, ((g + 3) % 4) // 2, 0)
             if okp(g - 1):
                 pe_xb(g - 1)
-            if okp(g - 6):
-                pe_m2(g - 6)
             if okp(g + 1):
                 dve_b(g + 1)

@@ -196,7 +196,7 @@ def tile_linearrecurrentunitcell_t_kernel(
 
         def pe_ut(c, hc):
             u_w = u_t[c][:].bitcast(F32)
-            ut = psum.tile([P, 2, 256], F32, tag="ut", name="ut")
+            ut = psum.tile([P, 2, 256], F32, tag="xn", name="ut", bufs=2)
             for jj in range(2):
                 j = 2 * hc + jj
                 for u in range(2):
@@ -208,7 +208,7 @@ def tile_linearrecurrentunitcell_t_kernel(
         def pe_st(c, u, which):
             src_t, tg = ((sre_t, "str"), (sim_t, "sti"))[which]
             s_w = src_t[c][:].bitcast(F32)
-            st = psum.tile([P, rows(c)], F32, tag=tg, name=tg)
+            st = psum.tile([P, rows(c)], F32, tag=tg, name=tg, bufs=1 + which)
             for j in range(mt(c)):
                 nc.tensor.transpose(st[:, j * P:(j + 1) * P], s_w[:, j * 256 + u * P:j * 256 + (u + 1) * P], ident[:])
             st_t[(c, u, which)] = st[:].bitcast(BF16).rearrange("p (m e) -> p m e", e=2)
@@ -397,10 +397,10 @@ def tile_linearrecurrentunitcell_t_kernel(
             if k == 3 and ok(c):
                 cast_x(c, 0, "g")
                 cast_x(c, 1, "a" if c == NCH - 1 else "g")
-            if okp(g - 2):
-                act_xn(g - 2)
             if ut_at(g) is not None:
                 act_ut(ut_at(g)[0], ut_at(g)[1])
+            if okp(g - 2):
+                act_xn(g - 2)
             if k == 2 and c >= 0:
                 if ok(c + 3):
                     load_s(c + 3)
@@ -409,8 +409,6 @@ def tile_linearrecurrentunitcell_t_kernel(
             if k == 1 and ok(c - 1):
                 store(out_1, c - 1, xo_t[c - 1][0])
                 store(out_2, c - 1, xo_t[c - 1][1])
-            if okp(g + 1) and (g + 1) % 2 == 0:
-                pe_st((g + 1) // 4, ((g + 1) % 4) // 2, 1)
             if okp(g + 1):
                 pe_m1(g + 1)
             if okp(g + 1 - YLAG):
@@ -419,6 +417,7 @@ def tile_linearrecurrentunitcell_t_kernel(
                 pe_ut(ut_at(g + 1)[0], ut_at(g + 1)[1])
             if okp(g + 3) and (g + 3) % 2 == 0:
                 pe_st((g + 3) // 4, ((g + 3) % 4) // 2, 0)
+                pe_st((g + 3) // 4, ((g + 3) % 4) // 2, 1)
             if okp(g - 1):
                 pe_xb(g - 1)
             if okp(g + 1):

@@ -27,6 +27,7 @@ NPL = 4 * NCH
 OFFS = [sum(CHUNKS[:c]) for c in range(NCH)]
 assert sum(CHUNKS) == ROWS
 YLAG = 7
+Y_OFF = 2
 KQ = 2
 
 
@@ -196,7 +197,7 @@ def tile_linearrecurrentunitcell_t_kernel(
 
         def pe_ut(c, hc):
             u_w = u_t[c][:].bitcast(F32)
-            ut = psum.tile([P, 2, 256], F32, tag="xn", name="ut", bufs=2)
+            ut = psum.tile([P, 2, 256], F32, tag="ut", name="ut")
             for jj in range(2):
                 j = 2 * hc + jj
                 for u in range(2):
@@ -208,7 +209,7 @@ def tile_linearrecurrentunitcell_t_kernel(
         def pe_st(c, u, which):
             src_t, tg = ((sre_t, "str"), (sim_t, "sti"))[which]
             s_w = src_t[c][:].bitcast(F32)
-            st = psum.tile([P, rows(c)], F32, tag=tg, name=tg, bufs=1 + which)
+            st = psum.tile([P, rows(c)], F32, tag=tg, name=tg)
             for j in range(mt(c)):
                 nc.tensor.transpose(st[:, j * P:(j + 1) * P], s_w[:, j * 256 + u * P:j * 256 + (u + 1) * P], ident[:])
             st_t[(c, u, which)] = st[:].bitcast(BF16).rearrange("p (m e) -> p m e", e=2)
@@ -332,7 +333,11 @@ def tile_linearrecurrentunitcell_t_kernel(
                 return
             if j == 0:
                 yo_t[c] = work.tile([P, mt(c), WIDTH], F32, tag="yo", name="yo")
-            nc.vector.tensor_tensor(out=yo_t[c][:, j, :], in0=yy_t[yi][:], in1=du_t[c][:, j, :], op=ALU.add)
+            if mt(c) == 4 and j == Y_OFF:
+                nc.scalar.copy(out=yo_t[c][:, j, :], in_=yy_t[yi][:])
+                nc.gpsimd.tensor_tensor(out=yo_t[c][:, j, :], in0=yo_t[c][:, j, :], in1=du_t[c][:, j, :], op=ALU.add)
+            else:
+                nc.vector.tensor_tensor(out=yo_t[c][:, j, :], in0=yy_t[yi][:], in1=du_t[c][:, j, :], op=ALU.add)
             if j == mt(c) - 1:
                 store(out_0, c, yo_t[c])
 
@@ -346,15 +351,17 @@ def tile_linearrecurrentunitcell_t_kernel(
             )
             du_t[c] = du
 
-        def cast_x(c, ri, eng):
+        def cast_x(c, ri, engs):
             tg = ("gxre", "gxim")[ri]
             gx = work.tile([P, 4 * rows(c)], BF16, tag=tg, name=tg, align_bytes=64)
-            dst = gx[:].rearrange("p (m t) -> p m t", t=4)
-            src = xT_t[c][ri][:].rearrange("p t m -> p m t")
-            if eng == "a":
-                nc.scalar.copy(out=dst, in_=src)
-            else:
-                nc.gpsimd.tensor_scalar(out=dst, in0=src, scalar1=1.0, scalar2=0.0, op0=ALU.mult, op1=ALU.add)
+            part = rows(c) // len(engs)
+            for i, eng in enumerate(engs):
+                dst = gx[:, 4 * part * i:4 * part * (i + 1)].rearrange("p (m t) -> p m t", t=4)
+                src = xT_t[c][ri][:, :, part * i:part * (i + 1)].rearrange("p t m -> p m t")
+                if eng == "a":
+                    nc.scalar.copy(out=dst, in_=src)
+                else:
+                    nc.gpsimd.tensor_scalar(out=dst, in0=src, scalar1=1.0, scalar2=0.0, op0=ALU.mult, op1=ALU.add)
             gx_t[(c, ri)] = gx
 
         def store(dram, c, src):
@@ -396,11 +403,11 @@ def tile_linearrecurrentunitcell_t_kernel(
                 pool_du(c)
             if k == 3 and ok(c):
                 cast_x(c, 0, "g")
-                cast_x(c, 1, "a" if c == NCH - 1 else "g")
-            if ut_at(g) is not None:
-                act_ut(ut_at(g)[0], ut_at(g)[1])
+                cast_x(c, 1, "a" if c == NCH - 1 else "ga")
             if okp(g - 2):
                 act_xn(g - 2)
+            if ut_at(g) is not None:
+                act_ut(ut_at(g)[0], ut_at(g)[1])
             if k == 2 and c >= 0:
                 if ok(c + 3):
                     load_s(c + 3)
@@ -409,6 +416,8 @@ def tile_linearrecurrentunitcell_t_kernel(
             if k == 1 and ok(c - 1):
                 store(out_1, c - 1, xo_t[c - 1][0])
                 store(out_2, c - 1, xo_t[c - 1][1])
+            if okp(g + 1) and (g + 1) % 2 == 0:
+                pe_st((g + 1) // 4, ((g + 1) % 4) // 2, 1)
             if okp(g + 1):
                 pe_m1(g + 1)
             if okp(g + 1 - YLAG):
@@ -417,7 +426,6 @@ def tile_linearrecurrentunitcell_t_kernel(
                 pe_ut(ut_at(g + 1)[0], ut_at(g + 1)[1])
             if okp(g + 3) and (g + 3) % 2 == 0:
                 pe_st((g + 3) // 4, ((g + 3) % 4) // 2, 0)
-                pe_st((g + 3) // 4, ((g + 3) % 4) // 2, 1)
             if okp(g - 1):
                 pe_xb(g - 1)
             if okp(g + 1):

@@ -27,7 +27,7 @@ NPL = 4 * NCH
 OFFS = [sum(CHUNKS[:c]) for c in range(NCH)]
 assert sum(CHUNKS) == ROWS
 YLAG = 7
-Y_OFF = 2
+Y_OFF = -1
 KQ = 2
 
 

@@ -27,7 +27,6 @@ NPL = 4 * NCH
 OFFS = [sum(CHUNKS[:c]) for c in range(NCH)]
 assert sum(CHUNKS) == ROWS
 YLAG = 7
-Y_OFF = -1
 KQ = 2
 
 
@@ -214,19 +213,22 @@ def tile_linearrecurrentunitcell_t_kernel(
                 nc.tensor.transpose(st[:, j * P:(j + 1) * P], s_w[:, j * 256 + u * P:j * 256 + (u + 1) * P], ident[:])
             st_t[(c, u, which)] = st[:].bitcast(BF16).rearrange("p (m e) -> p m e", e=2)
 
-        def pe_m1(g):
+        def pe_m1_pass(g, ri):
             c, t = divmod(g, 4)
             uc, us = uq_t[c]
+            cd, sc = b_cd[ri]
+            nc.tensor.matmul_mx(
+                out=pp_t[(g, ri)][:],
+                lhsT=cd[:, t * P:(t + 1) * P].bitcast(FP8X4), lhsT_scale=sc[:, t * P:(t + 1) * P],
+                rhs=uc[:].bitcast(FP8X4), rhs_scale=us[:],
+                start=True, stop=True,
+            )
+
+        def pe_m1(g):
             for ri in range(2):
-                cd, sc = b_cd[ri]
-                pp = psum.tile([P, rows(c)], F32, tag="pp", name="pp", bufs=2)
-                nc.tensor.matmul_mx(
-                    out=pp[:],
-                    lhsT=cd[:, t * P:(t + 1) * P].bitcast(FP8X4), lhsT_scale=sc[:, t * P:(t + 1) * P],
-                    rhs=uc[:].bitcast(FP8X4), rhs_scale=us[:],
-                    start=True, stop=True,
-                )
-                pp_t[(g, ri)] = pp
+                pp_t[(g, ri)] = psum.tile([P, rows(g // 4)], F32, tag="pp", name="pp", bufs=2)
+                for rep in range(2):
+                    pe_m1_pass(g, ri)
 
         def pe_xb(q):
             c, r = divmod(q, 4)
@@ -333,11 +335,7 @@ def tile_linearrecurrentunitcell_t_kernel(
                 return
             if j == 0:
                 yo_t[c] = work.tile([P, mt(c), WIDTH], F32, tag="yo", name="yo")
-            if mt(c) == 4 and j == Y_OFF:
-                nc.scalar.copy(out=yo_t[c][:, j, :], in_=yy_t[yi][:])
-                nc.gpsimd.tensor_tensor(out=yo_t[c][:, j, :], in0=yo_t[c][:, j, :], in1=du_t[c][:, j, :], op=ALU.add)
-            else:
-                nc.vector.tensor_tensor(out=yo_t[c][:, j, :], in0=yy_t[yi][:], in1=du_t[c][:, j, :], op=ALU.add)
+            nc.vector.tensor_tensor(out=yo_t[c][:, j, :], in0=yy_t[yi][:], in1=du_t[c][:, j, :], op=ALU.add)
             if j == mt(c) - 1:
                 store(out_0, c, yo_t[c])
 
@@ -351,17 +349,15 @@ def tile_linearrecurrentunitcell_t_kernel(
             )
             du_t[c] = du
 
-        def cast_x(c, ri, engs):
+        def cast_x(c, ri, eng):
             tg = ("gxre", "gxim")[ri]
             gx = work.tile([P, 4 * rows(c)], BF16, tag=tg, name=tg, align_bytes=64)
-            part = rows(c) // len(engs)
-            for i, eng in enumerate(engs):
-                dst = gx[:, 4 * part * i:4 * part * (i + 1)].rearrange("p (m t) -> p m t", t=4)
-                src = xT_t[c][ri][:, :, part * i:part * (i + 1)].rearrange("p t m -> p m t")
-                if eng == "a":
-                    nc.scalar.copy(out=dst, in_=src)
-                else:
-                    nc.gpsimd.tensor_scalar(out=dst, in0=src, scalar1=1.0, scalar2=0.0, op0=ALU.mult, op1=ALU.add)
+            dst = gx[:].rearrange("p (m t) -> p m t", t=4)
+            src = xT_t[c][ri][:].rearrange("p t m -> p m t")
+            if eng == "a":
+                nc.scalar.copy(out=dst, in_=src)
+            else:
+                nc.gpsimd.tensor_scalar(out=dst, in0=src, scalar1=1.0, scalar2=0.0, op0=ALU.mult, op1=ALU.add)
             gx_t[(c, ri)] = gx
 
         def store(dram, c, src):
@@ -403,7 +399,7 @@ def tile_linearrecurrentunitcell_t_kernel(
                 pool_du(c)
             if k == 3 and ok(c):
                 cast_x(c, 0, "g")
-                cast_x(c, 1, "a" if c == NCH - 1 else "ga")
+                cast_x(c, 1, "a" if c == NCH - 1 else "g")
             if okp(g - 2):
                 act_xn(g - 2)
             if ut_at(g) is not None:
@@ -420,7 +416,7 @@ def tile_linearrecurrentunitcell_t_kernel(
                 pe_st((g + 1) // 4, ((g + 1) % 4) // 2, 1)
             if okp(g + 1):
                 pe_m1(g + 1)
-            if okp(g + 1 - YLAG):
+            if okp(g + 1 - YLAG) and k != KQ:
                 pe_m2(g + 1 - YLAG, g >= NPL - 1)
             if ut_at(g + 1) is not None:
                 pe_ut(ut_at(g + 1)[0], ut_at(g + 1)[1])
@@ -428,5 +424,11 @@ def tile_linearrecurrentunitcell_t_kernel(
                 pe_st((g + 3) // 4, ((g + 3) % 4) // 2, 0)
             if okp(g - 1):
                 pe_xb(g - 1)
+            if k == KQ:
+                if okp(g + 1):
+                    pe_m1_pass(g + 1, 0)
+                    pe_m1_pass(g + 1, 1)
+                if okp(g + 1 - YLAG):
+                    pe_m2(g + 1 - YLAG, g >= NPL - 1)
             if okp(g + 1):
                 dve_b(g + 1)

@@ -27,6 +27,7 @@ NPL = 4 * NCH
 OFFS = [sum(CHUNKS[:c]) for c in range(NCH)]
 assert sum(CHUNKS) == ROWS
 YLAG = 7
+Y_OFF = 2
 KQ = 2
 
 
@@ -196,7 +197,7 @@ def tile_linearrecurrentunitcell_t_kernel(
 
         def pe_ut(c, hc):
             u_w = u_t[c][:].bitcast(F32)
-            ut = psum.tile([P, 2, 256], F32, tag="ut", name="ut")
+            ut = psum.tile([P, 2, 256], F32, tag="xn", name="ut", bufs=2)
             for jj in range(2):
                 j = 2 * hc + jj
                 for u in range(2):
@@ -208,27 +209,24 @@ def tile_linearrecurrentunitcell_t_kernel(
         def pe_st(c, u, which):
             src_t, tg = ((sre_t, "str"), (sim_t, "sti"))[which]
             s_w = src_t[c][:].bitcast(F32)
-            st = psum.tile([P, rows(c)], F32, tag=tg, name=tg)
+            st = psum.tile([P, rows(c)], F32, tag=tg, name=tg, bufs=1 + which)
             for j in range(mt(c)):
                 nc.tensor.transpose(st[:, j * P:(j + 1) * P], s_w[:, j * 256 + u * P:j * 256 + (u + 1) * P], ident[:])
             st_t[(c, u, which)] = st[:].bitcast(BF16).rearrange("p (m e) -> p m e", e=2)
 
-        def pe_m1_pass(g, ri):
+        def pe_m1(g):
             c, t = divmod(g, 4)
             uc, us = uq_t[c]
-            cd, sc = b_cd[ri]
-            nc.tensor.matmul_mx(
-                out=pp_t[(g, ri)][:],
-                lhsT=cd[:, t * P:(t + 1) * P].bitcast(FP8X4), lhsT_scale=sc[:, t * P:(t + 1) * P],
-                rhs=uc[:].bitcast(FP8X4), rhs_scale=us[:],
-                start=True, stop=True,
-            )
-
-        def pe_m1(g):
             for ri in range(2):
-                pp_t[(g, ri)] = psum.tile([P, rows(g // 4)], F32, tag="pp", name="pp", bufs=2)
-                for rep in range(2):
-                    pe_m1_pass(g, ri)
+                cd, sc = b_cd[ri]
+                pp = psum.tile([P, rows(c)], F32, tag="pp", name="pp", bufs=2)
+                nc.tensor.matmul_mx(
+                    out=pp[:],
+                    lhsT=cd[:, t * P:(t + 1) * P].bitcast(FP8X4), lhsT_scale=sc[:, t * P:(t + 1) * P],
+                    rhs=uc[:].bitcast(FP8X4), rhs_scale=us[:],
+                    start=True, stop=True,
+                )
+                pp_t[(g, ri)] = pp
 
         def pe_xb(q):
             c, r = divmod(q, 4)
@@ -335,7 +333,11 @@ def tile_linearrecurrentunitcell_t_kernel(
                 return
             if j == 0:
                 yo_t[c] = work.tile([P, mt(c), WIDTH], F32, tag="yo", name="yo")
-            nc.vector.tensor_tensor(out=yo_t[c][:, j, :], in0=yy_t[yi][:], in1=du_t[c][:, j, :], op=ALU.add)
+            if mt(c) == 4 and j == Y_OFF:
+                nc.scalar.copy(out=yo_t[c][:, j, :], in_=yy_t[yi][:])
+                nc.gpsimd.tensor_tensor(out=yo_t[c][:, j, :], in0=yo_t[c][:, j, :], in1=du_t[c][:, j, :], op=ALU.add)
+            else:
+                nc.vector.tensor_tensor(out=yo_t[c][:, j, :], in0=yy_t[yi][:], in1=du_t[c][:, j, :], op=ALU.add)
             if j == mt(c) - 1:
                 store(out_0, c, yo_t[c])
 
@@ -349,15 +351,17 @@ def tile_linearrecurrentunitcell_t_kernel(
             )
             du_t[c] = du
 
-        def cast_x(c, ri, eng):
+        def cast_x(c, ri, engs):
             tg = ("gxre", "gxim")[ri]
             gx = work.tile([P, 4 * rows(c)], BF16, tag=tg, name=tg, align_bytes=64)
-            dst = gx[:].rearrange("p (m t) -> p m t", t=4)
-            src = xT_t[c][ri][:].rearrange("p t m -> p m t")
-            if eng == "a":
-                nc.scalar.copy(out=dst, in_=src)
-            else:
-                nc.gpsimd.tensor_scalar(out=dst, in0=src, scalar1=1.0, scalar2=0.0, op0=ALU.mult, op1=ALU.add)
+            part = rows(c) // len(engs)
+            for i, eng in enumerate(engs):
+                dst = gx[:, 4 * part * i:4 * part * (i + 1)].rearrange("p (m t) -> p m t", t=4)
+                src = xT_t[c][ri][:, :, part * i:part * (i + 1)].rearrange("p t m -> p m t")
+                if eng == "a":
+                    nc.scalar.copy(out=dst, in_=src)
+                else:
+                    nc.gpsimd.tensor_scalar(out=dst, in0=src, scalar1=1.0, scalar2=0.0, op0=ALU.mult, op1=ALU.add)
             gx_t[(c, ri)] = gx
 
         def store(dram, c, src):
@@ -399,11 +403,11 @@ def tile_linearrecurrentunitcell_t_kernel(
                 pool_du(c)
             if k == 3 and ok(c):
                 cast_x(c, 0, "g")
-                cast_x(c, 1, "a" if c == NCH - 1 else "g")
-            if okp(g - 2):
-                act_xn(g - 2)
+                cast_x(c, 1, "a" if c == NCH - 1 else "ga")
             if ut_at(g) is not None:
                 act_ut(ut_at(g)[0], ut_at(g)[1])
+            if okp(g - 2):
+                act_xn(g - 2)
             if k == 2 and c >= 0:
                 if ok(c + 3):
                     load_s(c + 3)
@@ -412,23 +416,16 @@ def tile_linearrecurrentunitcell_t_kernel(
             if k == 1 and ok(c - 1):
                 store(out_1, c - 1, xo_t[c - 1][0])
                 store(out_2, c - 1, xo_t[c - 1][1])
-            if okp(g + 1) and (g + 1) % 2 == 0:
-                pe_st((g + 1) // 4, ((g + 1) % 4) // 2, 1)
             if okp(g + 1):
                 pe_m1(g + 1)
-            if okp(g + 1 - YLAG) and k != KQ:
+            if okp(g + 1 - YLAG):
                 pe_m2(g + 1 - YLAG, g >= NPL - 1)
             if ut_at(g + 1) is not None:
                 pe_ut(ut_at(g + 1)[0], ut_at(g + 1)[1])
             if okp(g + 3) and (g + 3) % 2 == 0:
                 pe_st((g + 3) // 4, ((g + 3) % 4) // 2, 0)
+                pe_st((g + 3) // 4, ((g + 3) % 4) // 2, 1)
             if okp(g - 1):
                 pe_xb(g - 1)
-            if k == KQ:
-                if okp(g + 1):
-                    pe_m1_pass(g + 1, 0)
-                    pe_m1_pass(g + 1, 1)
-                if okp(g + 1 - YLAG):
-                    pe_m2(g + 1 - YLAG, g >= NPL - 1)
             if okp(g + 1):
                 dve_b(g + 1)

from contextlib import ExitStack
import math

import concourse.mybir as mybir
from concourse.masks import make_identity

F32 = mybir.dt.float32
BF16 = mybir.dt.bfloat16
U32 = mybir.dt.uint32
U8 = mybir.dt.uint8
I32 = mybir.dt.int32
FP8X4 = mybir.dt.float8_e4m3fn_x4
ALU = mybir.AluOpType
ACTF = mybir.ActivationFunctionType

P = 128
ROWS = 4096
WIDTH = 512
FLOPS = 4 * 2 * ROWS * WIDTH * WIDTH

TWO_PI_HI = 6.28125
TWO_PI_LO = 2.0 * math.pi - 6.28125
CHUNKS = [512] * 7 + [256, 256]

NCH = len(CHUNKS)
NPL = 4 * NCH
OFFS = [sum(CHUNKS[:c]) for c in range(NCH)]
assert sum(CHUNKS) == ROWS
YLAG = 7
Y_OFF = 2
KQ = 2


def tile_linearrecurrentunitcell_t_kernel(
    tc, inputs, state_re, state_im, B_re, B_im, C_re, C_im, D, nu, theta, gamma, out_0, out_1, out_2
):
    nc = tc.nc
    with ExitStack() as ctx:
        ctx.enter_context(tc.manual_schedule())
        const = ctx.enter_context(tc.tile_pool(name="const", bufs=1))
        io = ctx.enter_context(tc.tile_pool(name="io", bufs=3))
        work = ctx.enter_context(tc.tile_pool(name="work", bufs=2))
        psum = ctx.enter_context(tc.psum_pool(name="psum", bufs=1))

        def ok(c):
            return 0 <= c < NCH

        def okp(g):
            return 0 <= g < NPL

        def rows(c):
            return CHUNKS[c]

        def mt(c):
            return CHUNKS[c] // P

        pr_nu = const.tile([P, 4], BF16, name="pr_nu")
        pr_th = const.tile([P, 4], BF16, name="pr_th")
        pr_ga = const.tile([P, 4], BF16, name="pr_ga")
        with nc.allow_non_contiguous_dma(reason="three vectors of 512 values, two neighbours a piece"):
            for dst, vec in ((pr_nu, nu), (pr_th, theta), (pr_ga, gamma)):
                nc.scalar.dma_start(
                    out=dst[:].rearrange("p (u e) -> p u e", u=2),
                    in_=vec.rearrange("(u q e) -> q u e", u=2, e=2),
                )
        dbc = const.tile([P, WIDTH], BF16, name="dbc")
        nc.scalar.dma_start(out=dbc[:], in_=D.partition_broadcast(P))

        u_t = {}
        sre_t = {}
        sim_t = {}

        def rows_of(dram, c):
            return dram[OFFS[c]:OFFS[c] + rows(c), :]

        def load_u(c):
            u_sb = io.tile([P, mt(c) * WIDTH], BF16, tag="u", name="u_sb", bufs=4)
            nc.sync.dma_start(out=u_sb[:], in_=rows_of(inputs, c).rearrange("(i j) k -> i (j k)", j=mt(c)))
            u_t[c] = u_sb

        def load_s(c):
            sre = io.tile([P, mt(c) * WIDTH], BF16, tag="sre", name="sre")
            nc.sync.dma_start(out=sre[:], in_=rows_of(state_re, c).rearrange("(i j) k -> i (j k)", j=mt(c)))
            sre_t[c] = sre
            sim = io.tile([P, mt(c) * WIDTH], BF16, tag="sim", name="sim")
            nc.sync.dma_start(out=sim[:], in_=rows_of(state_im, c).rearrange("(i j) k -> i (j k)", j=mt(c)))
            sim_t[c] = sim

        def load_w(w, nm, tg):
            raw = work.tile([P, 4 * WIDTH], BF16, tag=tg, name="raw_" + nm)
            nc.sync.dma_start(
                out=raw[:].rearrange("p (u x) -> p u x", u=2),
                in_=w.rearrange("(u q e) c -> q u (e c)", u=2, e=2),
            )
            return raw

        raw_bre = load_w(B_re, "bre", "xore")
        raw_bim = load_w(B_im, "bim", "xore")
        load_u(0)
        load_s(0)
        load_u(1)
        raw_cre = load_w(C_re, "cre", "xoim")
        raw_cim = load_w(C_im, "cim", "xoim")
        load_s(1)
        load_u(2)
        load_s(2)
        load_u(3)

        ident = const.tile([P, P], F32, name="ident")
        make_identity(nc, ident[:])

        def small(nm, dt=F32):
            return const.tile([P, 4], dt, name=nm)

        def quant(g_ap, nm):
            cd = const.tile([P, WIDTH], U32, name="cd_" + nm, align_bytes=64)
            sc = const.tile([P, WIDTH], U8, name="sc_" + nm, align_bytes=64)
            nc.vector.quantize_mx(out=cd[:].bitcast(FP8X4), scales=sc[:], in_=g_ap)
            return cd, sc

        def regroup_b(raw, nm):
            g = work.tile([P, 4 * WIDTH], BF16, tag="gxre", name="g_" + nm, align_bytes=64)
            src = raw[:].rearrange("p (t u q e) -> p u e q t", t=4, u=2, e=2)
            dst = g[:].rearrange("p (u e q t) -> p u e q t", u=2, e=2, t=4)
            for uu in range(2):
                nc.vector.tensor_copy(out=dst[:, uu], in_=src[:, uu])
            return g

        thf = small("thf")
        nc.vector.tensor_copy(out=thf[:], in_=pr_th[:])
        kq = small("kq")
        nc.vector.tensor_scalar_mul(out=kq[:], in0=thf[:], scalar1=1.0 / (2.0 * math.pi))
        ki = small("ki", I32)
        nc.vector.tensor_copy(out=ki[:], in_=kq[:])
        kf = small("kf")
        nc.vector.tensor_copy(out=kf[:], in_=ki[:])
        r1 = small("r1")
        nc.vector.scalar_tensor_tensor(out=r1[:], in0=kf[:], scalar=-TWO_PI_HI, in1=thf[:], op0=ALU.mult, op1=ALU.add)
        r2 = small("r2")
        nc.vector.scalar_tensor_tensor(out=r2[:], in0=kf[:], scalar=-TWO_PI_LO, in1=r1[:], op0=ALU.mult, op1=ALU.add)
        gam = small("gam")
        nc.vector.tensor_copy(out=gam[:], in_=pr_ga[:])
        e1 = small("e1")
        nc.scalar.activation(out=e1[:], in_=pr_nu[:], func=ACTF.Exp)
        mag = small("mag")
        nc.scalar.activation(out=mag[:], in_=e1[:], func=ACTF.Exp, scale=-1.0)
        sa = small("sa")
        nc.scalar.activation(out=sa[:], in_=r2[:], func=ACTF.Sin, scale=0.5)
        sb = small("sb")
        nc.scalar.activation(out=sb[:], in_=r2[:], func=ACTF.Sin, scale=0.25)

        g_bre = regroup_b(raw_bre, "bre")
        g_bim = regroup_b(raw_bim, "bim")

        sa2 = small("sa2")
        nc.vector.tensor_tensor(out=sa2[:], in0=sa[:], in1=sa[:], op=ALU.mult)
        cosr = small("cosr")
        nc.vector.tensor_scalar(out=cosr[:], in0=sa2[:], scalar1=-2.0, scalar2=1.0, op0=ALU.mult, op1=ALU.add)
        sb2 = small("sb2")
        nc.vector.tensor_tensor(out=sb2[:], in0=sb[:], in1=sb[:], op=ALU.mult)
        ch2 = small("ch2")
        nc.vector.tensor_scalar(out=ch2[:], in0=sb2[:], scalar1=-4.0, scalar2=2.0, op0=ALU.mult, op1=ALU.add)
        sinr = small("sinr")
        nc.vector.tensor_tensor(out=sinr[:], in0=sa[:], in1=ch2[:], op=ALU.mult)
        lam_re = small("lam_re")
        nc.vector.tensor_tensor(out=lam_re[:], in0=mag[:], in1=cosr[:], op=ALU.mult)
        lam_im = small("lam_im")
        nc.vector.tensor_tensor(out=lam_im[:], in0=mag[:], in1=sinr[:], op=ALU.mult)
        nlam_im = small("nlam_im")
        nc.vector.tensor_scalar_mul(out=nlam_im[:], in0=lam_im[:], scalar1=-1.0)

        b_cd = [quant(g_bre[:], "bre"), quant(g_bim[:], "bim")]
        c_cd = []

        gu_t = {}
        ut_t = {}
        uq_t = {}
        du_t = {}
        xT_t = {}
        gx_t = {}
        xq_t = {}
        xo_t = {}
        yo_t = {}
        st_t = {}
        pp_t = {}
        xn_t = {}
        yy_t = {}

        gu_t[1] = work.tile([P, 4 * rows(1)], BF16, tag="du", name="gu1", align_bytes=64)
        g_c = work.tile([P, 2, 4 * WIDTH], BF16, tag="du", name="g_c", align_bytes=64)
        for ri, (raw, sign) in enumerate(((raw_cre, 1.0), (raw_cim, -1.0))):
            nc.gpsimd.tensor_scalar(
                out=g_c[:, ri, :].rearrange("p (n t) -> p n t", t=4),
                in0=raw[:].rearrange("p (t n) -> p n t", t=4),
                scalar1=sign, scalar2=0.0, op0=ALU.mult, op1=ALU.add,
            )

        def pe_ut(c, hc):
            u_w = u_t[c][:].bitcast(F32)
            ut = psum.tile([P, 2, 256], F32, tag="xn", name="ut", bufs=2)
            for jj in range(2):
                j = 2 * hc + jj
                for u in range(2):
                    nc.tensor.transpose(
                        ut[:, u, jj * P:(jj + 1) * P], u_w[:, j * 256 + u * P:j * 256 + (u + 1) * P], ident[:]
                    )
            ut_t[(c, hc)] = ut

        def pe_st(c, u, which):
            src_t, tg = ((sre_t, "str"), (sim_t, "sti"))[which]
            s_w = src_t[c][:].bitcast(F32)
            st = psum.tile([P, rows(c)], F32, tag=tg, name=tg, bufs=1 + which)
            for j in range(mt(c)):
                nc.tensor.transpose(st[:, j * P:(j + 1) * P], s_w[:, j * 256 + u * P:j * 256 + (u + 1) * P], ident[:])
            st_t[(c, u, which)] = st[:].bitcast(BF16).rearrange("p (m e) -> p m e", e=2)

        def pe_m1(g):
            c, t = divmod(g, 4)
            uc, us = uq_t[c]
            for ri in range(2):
                cd, sc = b_cd[ri]
                pp = psum.tile([P, rows(c)], F32, tag="pp", name="pp", bufs=2)
                nc.tensor.matmul_mx(
                    out=pp[:],
                    lhsT=cd[:, t * P:(t + 1) * P].bitcast(FP8X4), lhsT_scale=sc[:, t * P:(t + 1) * P],
                    rhs=uc[:].bitcast(FP8X4), rhs_scale=us[:],
                    start=True, stop=True,
                )
                pp_t[(g, ri)] = pp

        def pe_xb(q):
            c, r = divmod(q, 4)
            u, jp = divmod(r, 2)
            if 2 * jp >= mt(c):
                return
            for ri in range(2):
                xn = psum.tile([P, 2, 2, P], F32, tag="xn", name="xn", bufs=2)
                for jj in range(2):
                    j = 2 * jp + jj
                    for e in range(2):
                        nc.tensor.transpose(xn[:, jj, e, :], xT_t[c][ri][:, 2 * u + e, j * P:(j + 1) * P], ident[:])
                xn_t[(q, ri)] = xn

        def pe_m2(yi, spare_banks):
            c, j = divmod(yi, 4)
            if j >= mt(c):
                return
            tg = "pp" if (spare_banks and yi % 3 != 0) else "yy"
            yy = psum.tile([P, WIDTH], F32, tag=tg, name="yy", bufs=(1 if tg == "yy" else 2))
            for ri in range(2):
                xc, xs = xq_t[(c, ri)]
                cd, sc = c_cd[ri]
                nc.tensor.matmul_mx(
                    out=yy[:],
                    lhsT=xc[:, j * P:(j + 1) * P].bitcast(FP8X4), lhsT_scale=xs[:, j * P:(j + 1) * P],
                    rhs=cd[:].bitcast(FP8X4), rhs_scale=sc[:],
                    start=(ri == 0), stop=(ri == 1),
                )
            yy_t[yi] = yy

        def act_ut(c, hc):
            if c not in gu_t:
                gu_t[c] = work.tile([P, 4 * rows(c)], BF16, tag="gu", name="gu", align_bytes=64)
            gu_w = gu_t[c][:].bitcast(F32).rearrange("p (m u) -> p m u", u=2)
            nc.scalar.copy(out=gu_w[:, hc * 256:(hc + 1) * 256, :], in_=ut_t[(c, hc)][:].rearrange("p u m -> p m u"))

        def act_a(g):
            c, t = divmod(g, 4)
            u, e = divmod(t, 2)
            if t == 0:
                xre = work.tile([P, 4, rows(c)], F32, tag="xTre", name="xTre", bufs=3)
                xim = work.tile([P, 4, rows(c)], F32, tag="xTim", name="xTim", bufs=3)
                xT_t[c] = (xre, xim)
            xre, xim = xT_t[c]
            s_re = st_t[(c, u, 0)]
            nc.scalar.activation(out=xre[:, t, :], in_=s_re[:, :, e], func=ACTF.Copy, scale=lam_re[:, t:t + 1])
            nc.scalar.activation(out=xim[:, t, :], in_=s_re[:, :, e], func=ACTF.Copy, scale=lam_im[:, t:t + 1])

        def act_xn(q):
            c, r = divmod(q, 4)
            u, jp = divmod(r, 2)
            if r == 0:
                xore = work.tile([P, mt(c), WIDTH], F32, tag="xore", name="xore")
                xoim = work.tile([P, mt(c), WIDTH], F32, tag="xoim", name="xoim")
                xo_t[c] = (xore, xoim)
            if 2 * jp >= mt(c):
                return
            for ri in range(2):
                nc.scalar.copy(
                    out=xo_t[c][ri][:, 2 * jp:2 * jp + 2, 256 * u:256 * u + 256].rearrange("p j (q e) -> p j q e", e=2),
                    in_=xn_t[(q, ri)][:].rearrange("p j e q -> p j q e"),
                )

        def dve_b(g):
            c, t = divmod(g, 4)
            u, e = divmod(t, 2)
            xre, xim = xT_t[c]
            s_im = st_t[(c, u, 1)]
            nc.vector.scalar_tensor_tensor(
                out=xre[:, t, :], in0=s_im[:, :, e], scalar=nlam_im[:, t:t + 1], in1=xre[:, t, :],
                op0=ALU.mult, op1=ALU.add,
            )
            nc.vector.scalar_tensor_tensor(
                out=xim[:, t, :], in0=s_im[:, :, e], scalar=lam_re[:, t:t + 1], in1=xim[:, t, :],
                op0=ALU.mult, op1=ALU.add,
            )

        def dve_x(g):
            c, t = divmod(g, 4)
            for ri in range(2):
                x = xT_t[c][ri]
                nc.vector.scalar_tensor_tensor(
                    out=x[:, t, :], in0=pp_t[(g, ri)][:], scalar=gam[:, t:t + 1], in1=x[:, t, :],
                    op0=ALU.mult, op1=ALU.add,
                )

        def dve_qu(c):
            uc = work.tile([P, rows(c)], U32, tag="uc", name="uc", align_bytes=64)
            us = work.tile([P, rows(c)], U8, tag="us", name="us", align_bytes=64)
            nc.vector.quantize_mx(out=uc[:].bitcast(FP8X4), scales=us[:], in_=gu_t[c][:])
            uq_t[c] = (uc, us)

        def dve_qx(c, ri):
            tg = ("re", "im")[ri]
            xc = work.tile([P, rows(c)], U32, tag="xc" + tg, name="xc" + tg, align_bytes=64)
            xs = work.tile([P, rows(c)], U8, tag="xs" + tg, name="xs" + tg, align_bytes=64)
            nc.vector.quantize_mx(out=xc[:].bitcast(FP8X4), scales=xs[:], in_=gx_t[(c, ri)][:])
            xq_t[(c, ri)] = (xc, xs)

        def dve_y(yi):
            c, j = divmod(yi, 4)
            if j >= mt(c):
                return
            if j == 0:
                yo_t[c] = work.tile([P, mt(c), WIDTH], F32, tag="yo", name="yo")
            if mt(c) == 4 and j == Y_OFF:
                nc.scalar.copy(out=yo_t[c][:, j, :], in_=yy_t[yi][:])
                nc.gpsimd.tensor_tensor(out=yo_t[c][:, j, :], in0=yo_t[c][:, j, :], in1=du_t[c][:, j, :], op=ALU.add)
            else:
                nc.vector.tensor_tensor(out=yo_t[c][:, j, :], in0=yy_t[yi][:], in1=du_t[c][:, j, :], op=ALU.add)
            if j == mt(c) - 1:
                store(out_0, c, yo_t[c])

        def pool_du(c):
            du = work.tile([P, mt(c), WIDTH], F32, tag="du", name="du", align_bytes=64)
            nc.gpsimd.tensor_tensor(
                out=du[:],
                in0=u_t[c][:].rearrange("p (j k) -> p j k", j=mt(c)),
                in1=dbc[:].unsqueeze(1).to_broadcast([P, mt(c), WIDTH]),
                op=ALU.mult,
            )
            du_t[c] = du

        def cast_x(c, ri, engs):
            tg = ("gxre", "gxim")[ri]
            gx = work.tile([P, 4 * rows(c)], BF16, tag=tg, name=tg, align_bytes=64)
            part = rows(c) // len(engs)
            for i, eng in enumerate(engs):
                dst = gx[:, 4 * part * i:4 * part * (i + 1)].rearrange("p (m t) -> p m t", t=4)
                src = xT_t[c][ri][:, :, part * i:part * (i + 1)].rearrange("p t m -> p m t")
                if eng == "a":
                    nc.scalar.copy(out=dst, in_=src)
                else:
                    nc.gpsimd.tensor_scalar(out=dst, in0=src, scalar1=1.0, scalar2=0.0, op0=ALU.mult, op1=ALU.add)
            gx_t[(c, ri)] = gx

        def store(dram, c, src):
            nc.sync.dma_start(out=rows_of(dram, c).rearrange("(i j) h -> i j h", j=mt(c)), in_=src[:])

        def ut_at(g):
            c, k = divmod(g, 4)
            w = None
            if g in (-7, -5):
                w = (0, (g + 7) // 2)
            elif g in (0, 1):
                w = (1, g)
            elif c >= 0 and k >= 2 and ok(c + 2):
                w = (c + 2, k - 2)
            if w is not None and 2 * w[1] >= mt(w[0]):
                w = None
            return w

        for g in range(-8, NPL + YLAG):
            c, k = divmod(g, 4)
            if okp(g):
                dve_x(g)
            if g == -4:
                dve_qu(0)
            if k == KQ:
                if ok(c - 1):
                    dve_qx(c - 1, 0)
                    dve_qx(c - 1, 1)
                if c == 1:
                    c_cd.append(quant(g_c[:, 0, :], "cre"))
                    c_cd.append(quant(g_c[:, 1, :], "cim"))
                if c >= 0 and ok(c + 1):
                    dve_qu(c + 1)
            if okp(g - YLAG):
                dve_y(g - YLAG)
            if okp(g + 2):
                act_a(g + 2)
            if k == KQ and ok(c):
                pool_du(c)
            if k == 3 and ok(c):
                cast_x(c, 0, "g")
                cast_x(c, 1, "a" if c == NCH - 1 else "ga")
            if ut_at(g) is not None:
                act_ut(ut_at(g)[0], ut_at(g)[1])
            if okp(g - 2):
                act_xn(g - 2)
            if k == 2 and c >= 0:
                if ok(c + 3):
                    load_s(c + 3)
                if ok(c + 4):
                    load_u(c + 4)
            if k == 1 and ok(c - 1):
                store(out_1, c - 1, xo_t[c - 1][0])
                store(out_2, c - 1, xo_t[c - 1][1])
            if okp(g + 1):
                pe_m1(g + 1)
            if okp(g + 1 - YLAG):
                pe_m2(g + 1 - YLAG, g >= NPL - 1)
            if ut_at(g + 1) is not None:
                pe_ut(ut_at(g + 1)[0], ut_at(g + 1)[1])
            if okp(g + 3) and (g + 3) % 2 == 0:
                pe_st((g + 3) // 4, ((g + 3) % 4) // 2, 0)
                pe_st((g + 3) // 4, ((g + 3) % 4) // 2, 1)
            if okp(g - 1):
                pe_xb(g - 1)
            if okp(g + 1):
                dve_b(g + 1)
